import numpy as np
import ml_dtypes


def mxq(x, axis, fmt="e4m3"):
    dtype, down = {"e4m3": (ml_dtypes.float8_e4m3fn, 7), "e5m2": (ml_dtypes.float8_e5m2, 14)}[fmt]
    v = np.moveaxis(np.asarray(x, np.float32).astype(ml_dtypes.bfloat16).astype(np.float64), axis, -1)
    blocks = v.reshape(v.shape[:-1] + (-1, 32))
    amax = np.abs(blocks).max(-1, keepdims=True)
    byte = np.maximum(np.where(amax > 0, np.frexp(amax)[1] - 1 + 127, 0) - down, 1)
    scale = np.exp2(byte - 127.0)
    codes = (blocks / scale).astype(np.float32).astype(dtype).astype(np.float64)
    return np.moveaxis((codes * scale).reshape(v.shape), -1, axis)


WIDE = False


def mx_kscale(k):
    if not WIDE:
        return np.ones(k)
    levels = np.array([10, -10, 5, -5, 0])
    a = np.random.permutation(np.resize(levels, k // 512 * 4)).reshape(k // 512, 4)
    idx = np.arange(k)
    return np.exp2(a[idx // 512, idx % 128 // 32])


BF16 = ml_dtypes.bfloat16


def bf(x):
    return np.asarray(x, np.float32).astype(BF16)


def f64(x):
    return np.asarray(x).astype(np.float64)


E2M1 = np.array([0.0, 0.5, 1.0, 1.5, 2.0, 3.0, 4.0, 6.0, -0.0, -0.5, -1.0, -1.5, -2.0, -3.0, -4.0, -6.0])


def pack_weight(w, fmt):
    k, n = w.shape
    w = f64(bf(w)).reshape(k // 32, 32, n)
    amax = np.abs(w).max(1)
    if fmt == "e4m3":
        byte = np.frexp(amax)[1] - 1 + 127 - 7
    else:
        mant, ex = np.frexp(amax / 6.0)
        byte = np.where(mant > 0.5, ex, ex - 1) + 127
    byte = np.clip(np.where(amax > 0, byte, 1), 1, 254)
    scaled = (w * np.exp2(127.0 - byte)[:, None, :]).reshape(k, n).astype(np.float32)
    by_word = np.ascontiguousarray(scaled.reshape(k // 512, 128, 4, n).transpose(0, 1, 3, 2))
    if fmt == "e4m3":
        words = by_word.astype(ml_dtypes.float8_e4m3fn).view(np.uint8)
    else:
        c = by_word.astype(ml_dtypes.float4_e2m1fn).view(np.uint8) & 0xF
        words = c[..., 0::2] | (c[..., 1::2] << 4)
    return np.ascontiguousarray(words), np.ascontiguousarray(byte.astype(np.uint8).reshape(k // 512, 16, n))


def unpack_weight(words, scales, fmt):
    g, p, n, _ = words.shape
    if fmt == "e4m3":
        vals = np.ascontiguousarray(words).view(ml_dtypes.float8_e4m3fn).astype(np.float64)
    else:
        nib = np.empty((g, p, n, 4), np.uint8)
        nib[..., 0::2] = words & 0xF
        nib[..., 1::2] = words >> 4
        vals = E2M1[nib]
    vals = vals * np.repeat(np.exp2(scales.astype(np.float64) - 127.0), 8, axis=1)[..., None]
    return vals.transpose(0, 1, 3, 2).reshape(g * 512, n)

def pack4(w):
    words, scales = pack_weight(w, "e2m1")
    return words.reshape(words.shape[0], 128, -1), scales


def unpack4(words, scales):
    return unpack_weight(words.reshape(words.shape[0], 128, -1, 2), scales, "e2m1")


B, I, H = 768, 512, 128


def sigmoid(v):
    return 1.0 / (1.0 + np.exp(-v))


def setup_inputs():
    s = mx_kscale(I)
    input_ = bf(np.random.standard_normal((B, I)) * s)
    c_input = bf(np.random.standard_normal((B, 1, H)))
    h_0 = bf(np.random.standard_normal((B, H)))
    weight_ih_words, weight_ih_scales = pack4(np.random.standard_normal((I, 3 * H)) / np.sqrt(I) / s[:, None])
    weight_hh = bf(np.random.standard_normal((H, 3 * H)) / np.sqrt(H))
    alpha_weight_ih_words, alpha_weight_ih_scales = pack4(np.random.standard_normal((I, H)) / np.sqrt(I) / s[:, None])
    alpha_weight_hh = bf(np.random.standard_normal((H, H)) / np.sqrt(H))
    bias = bf(np.random.standard_normal(3 * H) * 0.5)
    alpha_bias = bf(np.random.standard_normal(H) * 0.5)
    return {
        "input_": input_,
        "c_input": c_input,
        "h_0": h_0,
        "weight_ih_words": weight_ih_words,
        "weight_ih_scales": weight_ih_scales,
        "weight_hh": weight_hh,
        "alpha_weight_ih_words": alpha_weight_ih_words,
        "alpha_weight_ih_scales": alpha_weight_ih_scales,
        "alpha_weight_hh": alpha_weight_hh,
        "bias": bias,
        "alpha_bias": alpha_bias,
    }


def reference(input_, c_input, h_0, weight_ih_words, weight_ih_scales, weight_hh, alpha_weight_ih_words, alpha_weight_ih_scales, alpha_weight_hh, bias, alpha_bias):
    xq = mxq(f64(input_), 1, "e4m3")
    wh_b = f64(h_0) @ f64(weight_hh) + f64(bias)
    wi = xq @ unpack4(weight_ih_words, weight_ih_scales)
    pre = wh_b + wi
    i_gate = sigmoid(pre[:, :H])
    o_gate = sigmoid(pre[:, H:2 * H])
    g = np.tanh(pre[:, 2 * H:])
    c_in = f64(c_input)[:, 0, :]
    alpha = sigmoid((xq @ unpack4(alpha_weight_ih_words, alpha_weight_ih_scales)) + f64(alpha_bias) + c_in @ f64(alpha_weight_hh))
    e_i = np.exp(i_gate)
    e_a = np.exp(alpha)
    denom = e_i + e_a
    w_i = e_i / denom
    w_a = e_a / denom
    c_1 = w_i * g + w_a * c_in
    h_1 = o_gate * np.tanh(c_1)
    return (h_1, c_1)

@@ -1,0 +1,239 @@
+from contextlib import ExitStack
+
+import concourse.mybir as mybir
+from concourse.masks import make_identity
+
+F32 = mybir.dt.float32
+BF16 = mybir.dt.bfloat16
+I32 = mybir.dt.int32
+U32 = mybir.dt.uint32
+U8 = mybir.dt.uint8
+FP8X4 = mybir.dt.float8_e4m3fn_x4
+FP4X4 = mybir.dt.float4_e2m1fn_x4
+ACT = mybir.ActivationFunctionType
+ALU = mybir.AluOpType
+
+P = 128
+B = 768
+I = 512
+H = 128
+ROW_TILES = B // P
+GATES = 4 * H
+X_LOADS = 2
+TILES_PER_LOAD = ROW_TILES // X_LOADS
+GROUP = 2
+GROUPS = ROW_TILES // GROUP
+
+FLOPS = 2 * B * I * GATES + 2 * B * H * GATES
+
+
+def tile_multiinputlstmcell_pa_s_kernel(
+    tc,
+    input_,
+    c_input,
+    h_0,
+    weight_ih_words,
+    weight_ih_scales,
+    weight_hh,
+    alpha_weight_ih_words,
+    alpha_weight_ih_scales,
+    alpha_weight_hh,
+    bias,
+    alpha_bias,
+    out_0,
+    out_1,
+):
+    nc = tc.nc
+    COL_A = slice(0 * H, 1 * H)
+    COL_I = slice(1 * H, 2 * H)
+    COL_O = slice(2 * H, 3 * H)
+    COL_G = slice(3 * H, 4 * H)
+    COL_IOG = slice(1 * H, 4 * H)
+    COL_SIGMOID = slice(0, 3 * H)
+    x_rows = input_.rearrange("(p j) k -> p j k", j=ROW_TILES)
+    h_rows = h_0.rearrange("(p j) h -> p j h", j=ROW_TILES)
+    c_rows = c_input.rearrange("(p j) o h -> p j (o h)", j=ROW_TILES)
+    h1_rows = out_0.rearrange("(p j) h -> p j h", j=ROW_TILES)
+    c1_rows = out_1.rearrange("(p j) h -> p j h", j=ROW_TILES)
+
+    with ExitStack() as ctx:
+        keep = ctx.enter_context(tc.tile_pool(name="keep", bufs=1))
+        work = ctx.enter_context(tc.tile_pool(name="work", bufs=ROW_TILES))
+        turn_ps = ctx.enter_context(tc.psum_pool(name="turn_ps", bufs=4))
+        plain_ps = ctx.enter_context(tc.psum_pool(name="plain_ps", bufs=2))
+        mx_ps = ctx.enter_context(tc.psum_pool(name="mx_ps", bufs=2))
+        ctx.enter_context(tc.manual_schedule())
+
+        bias_row = keep.tile([P, GATES], BF16)
+        nc.vector.memset(bias_row[:], 0.0)
+        ident_f32 = keep.tile([P, P], F32)
+        nc.vector.memset(ident_f32[:], 0.0)
+        make_identity(nc, ident_f32[:], nomemset=True)
+        w_scales = keep.tile([P, GATES], U8, align_bytes=64)
+        nc.vector.memset(w_scales[:].bitcast(I32), 0)
+        ones = keep.tile([P, P], BF16)
+        nc.vector.memset(ones[:], 1.0)
+        warm_in = keep.tile([P, 1], F32)
+        nc.vector.memset(warm_in[:], 0.0)
+        ident_bf16 = keep.tile([P, P], BF16)
+        nc.vector.tensor_copy(out=ident_bf16[:], in_=ident_f32[:])
+
+        h_sb = keep.tile([P, ROW_TILES, H], BF16)
+        nc.sync.dma_start(out=h_sb[:], in_=h_rows)
+        c_sb = keep.tile([P, ROW_TILES, H], BF16)
+        nc.scalar.dma_start(out=c_sb[:], in_=c_rows)
+        nc.scalar.dma_start(out=bias_row[0:1, COL_IOG], in_=bias.unsqueeze(0))
+        nc.scalar.dma_start(out=bias_row[0:1, COL_A], in_=alpha_bias.unsqueeze(0))
+        w_plain = keep.tile([P, GATES], BF16)
+        nc.scalar.dma_start(out=w_plain[:, COL_IOG], in_=weight_hh)
+        nc.scalar.dma_start(out=w_plain[:, COL_A], in_=alpha_weight_hh)
+        x_sb = []
+        for s in range(X_LOADS):
+            x_part = keep.tile([P, TILES_PER_LOAD, I], BF16, name="x_part%d" % s)
+            nc.sync.dma_start(
+                out=x_part[:], in_=x_rows[:, s * TILES_PER_LOAD : (s + 1) * TILES_PER_LOAD, :]
+            )
+            x_sb.append(x_part)
+        w_words = keep.tile([P, 2 * GATES], U8, align_bytes=64)
+        nc.sync.dma_start(
+            out=w_words[:, 2 * H : 2 * GATES].bitcast(I32), in_=weight_ih_words[0].bitcast(I32)
+        )
+        nc.sync.dma_start(
+            out=w_words[:, 0 : 2 * H].bitcast(I32), in_=alpha_weight_ih_words[0].bitcast(I32)
+        )
+        for scales, cols in ((weight_ih_scales, COL_IOG), (alpha_weight_ih_scales, COL_A)):
+            for q in range(4):
+                nc.sync.dma_start(
+                    out=w_scales[32 * q : 32 * q + 4, cols].bitcast(I32),
+                    in_=scales[0, 4 * q : 4 * q + 4, :].bitcast(I32),
+                )
+
+        warm_out = keep.tile([P, 1], F32)
+        nc.scalar.activation(out=warm_out[:], in_=warm_in[:], func=ACT.Sigmoid)
+
+        bias_all = keep.tile([P, GATES], F32)
+        x_codes = keep.tile([P, B], U32, align_bytes=64)
+        x_scales = keep.tile([P, B], U8, align_bytes=64)
+        hc_t = {}
+        plain_sb = {}
+        grouped = {}
+        acc = {}
+        gates = {}
+        g_minus_c = {}
+        w_i = {}
+        c_1 = {}
+        tanh_c1 = {}
+
+        def spread_biases():
+            bias_ps = plain_ps.tile([P, GATES], F32, tag="plain")
+            nc.tensor.matmul(out=bias_ps[:], lhsT=ones[:], rhs=bias_row[:], start=True, stop=True)
+            nc.vector.tensor_copy(out=bias_all[:], in_=bias_ps[:])
+
+        def turn_hc(j):
+            if not 0 <= j < ROW_TILES:
+                return
+            hc_ps = turn_ps.tile([P, 2, P], BF16, tag="turn")
+            nc.tensor.transpose(out=hc_ps[:, 0, :], in_=h_sb[:, j, :], identity=ident_bf16[:])
+            nc.tensor.transpose(out=hc_ps[:, 1, :], in_=c_sb[:, j, :], identity=ident_bf16[:])
+            hc_t[j] = work.tile([P, 2, P], BF16, name="hc_t")
+            nc.scalar.copy(out=hc_t[j][:], in_=hc_ps[:])
+
+        def plain_products(j):
+            if not 0 <= j < ROW_TILES:
+                return
+            plain = plain_ps.tile([P, GATES], F32, tag="plain")
+            nc.tensor.matmul(
+                out=plain[:, COL_IOG], lhsT=hc_t[j][:, 0, :], rhs=w_plain[:, COL_IOG], start=True, stop=True
+            )
+            nc.tensor.matmul(
+                out=plain[:, COL_A], lhsT=hc_t[j][:, 1, :], rhs=w_plain[:, COL_A], start=True, stop=True
+            )
+            plain_sb[j] = work.tile([P, GATES], F32, name="plain_sb")
+            nc.vector.tensor_tensor(out=plain_sb[j][:], in0=plain[:], in1=bias_all[:], op=ALU.add)
+
+        def turn_x(j):
+            if not 0 <= j < ROW_TILES:
+                return
+            x_words = x_sb[j // TILES_PER_LOAD][:, j % TILES_PER_LOAD, :].bitcast(F32)
+            x_ps = turn_ps.tile([P, 2, P], F32, tag="turn")
+            for u in range(2):
+                nc.tensor.transpose(out=x_ps[:, u, :], in_=x_words[:, u : I // 2 : 2], identity=ident_f32[:])
+            grouped[j] = work.tile([P, P, 4], BF16, name="grouped", align_bytes=64)
+            nc.scalar.copy(
+                out=grouped[j][:].rearrange("p b t -> p (b t)").bitcast(F32).rearrange("p (b u) -> p b u", u=2),
+                in_=x_ps[:].rearrange("p u b -> p b u"),
+            )
+
+        def quantise(j):
+            if not 0 <= j < ROW_TILES:
+                return
+            rows = slice(j * P, (j + 1) * P)
+            nc.vector.quantize_mx(
+                out=x_codes[:, rows].bitcast(FP8X4),
+                scales=x_scales[:, rows],
+                in_=grouped[j][:].rearrange("p b t -> p (b t)"),
+            )
+
+        def mx_products(j):
+            if not 0 <= j < ROW_TILES:
+                return
+            rows = slice(j * P, (j + 1) * P)
+            acc[j] = mx_ps.tile([P, GATES], F32, name="acc")
+            nc.tensor.matmul_mx(
+                out=acc[j][:],
+                lhsT=x_codes[:, rows].bitcast(FP8X4),
+                lhsT_scale=x_scales[:, rows],
+                rhs=w_words[:].bitcast(FP4X4),
+                rhs_scale=w_scales[:],
+                start=True,
+                stop=True,
+            )
+
+        def four_gates(j):
+            pre = work.tile([P, GATES], F32)
+            nc.vector.tensor_tensor(out=pre[:], in0=acc[j][:], in1=plain_sb[j][:], op=ALU.add)
+            of_tile = gates[j // GROUP][:, j % GROUP, :]
+            nc.scalar.activation(out=of_tile[:, COL_SIGMOID], in_=pre[:, COL_SIGMOID], func=ACT.Sigmoid)
+            nc.scalar.activation(out=of_tile[:, COL_G], in_=pre[:, COL_G], func=ACT.Tanh)
+
+        turn_hc(0)
+        turn_hc(1)
+        spread_biases()
+        for j in range(ROW_TILES + 3):
+            turn_hc(j + 2)
+            plain_products(j)
+            turn_x(j - 2)
+            quantise(j - 3)
+
+        for g in range(GROUPS):
+            gates[g] = keep.tile([P, GROUP, GATES], F32, name="gates%d" % g)
+        mx_products(0)
+        mx_products(1)
+        for j in range(ROW_TILES):
+            four_gates(j)
+            mx_products(j + 2)
+
+        for g in range(GROUPS):
+            c_in = c_sb[:, g * GROUP : (g + 1) * GROUP, :]
+            i_minus_a = work.tile([P, GROUP, H], F32)
+            nc.vector.tensor_tensor(
+                out=i_minus_a[:], in0=gates[g][:, :, COL_I], in1=gates[g][:, :, COL_A], op=ALU.subtract
+            )
+            w_i[g] = work.tile([P, GROUP, H], F32, name="w_i")
+            nc.scalar.activation(out=w_i[g][:], in_=i_minus_a[:], func=ACT.Sigmoid)
+            g_minus_c[g] = work.tile([P, GROUP, H], F32, name="g_minus_c")
+            nc.vector.tensor_tensor(out=g_minus_c[g][:], in0=gates[g][:, :, COL_G], in1=c_in, op=ALU.subtract)
+        for g in range(GROUPS):
+            c_1[g] = work.tile([P, GROUP, H], F32, name="c_1")
+            nc.vector.tensor_tensor(out=c_1[g][:], in0=w_i[g][:], in1=g_minus_c[g][:], op=ALU.mult)
+        for g in range(GROUPS):
+            tiles = slice(g * GROUP, (g + 1) * GROUP)
+            nc.vector.tensor_tensor(out=c_1[g][:], in0=c_1[g][:], in1=c_sb[:, tiles, :], op=ALU.add)
+            nc.sync.dma_start(out=c1_rows[:, tiles, :], in_=c_1[g][:])
+            tanh_c1[g] = work.tile([P, GROUP, H], F32, name="tanh_c1")
+            nc.scalar.activation(out=tanh_c1[g][:], in_=c_1[g][:], func=ACT.Tanh)
+        for g in range(GROUPS):
+            tiles = slice(g * GROUP, (g + 1) * GROUP)
+            h_1 = work.tile([P, GROUP, H], F32)
+            nc.vector.tensor_tensor(out=h_1[:], in0=gates[g][:, :, COL_O], in1=tanh_c1[g][:], op=ALU.mult)
+            nc.sync.dma_start(out=h1_rows[:, tiles, :], in_=h_1[:])

@@ -78,15 +78,25 @@ def tile_multiinputlstmcell_pa_s_kernel(
         ident_bf16 = keep.tile([P, P], BF16)
         nc.vector.tensor_copy(out=ident_bf16[:], in_=ident_f32[:])
 
-        h_sb = keep.tile([P, ROW_TILES, H], BF16)
-        nc.sync.dma_start(out=h_sb[:], in_=h_rows)
-        c_sb = keep.tile([P, ROW_TILES, H], BF16)
-        nc.scalar.dma_start(out=c_sb[:], in_=c_rows)
+        h_first = keep.tile([P, GROUP, H], BF16)
+        nc.sync.dma_start(out=h_first[:], in_=h_rows[:, 0:GROUP, :])
+        c_first = keep.tile([P, GROUP, H], BF16)
+        nc.scalar.dma_start(out=c_first[:], in_=c_rows[:, 0:GROUP, :])
         nc.scalar.dma_start(out=bias_row[0:1, COL_IOG], in_=bias.unsqueeze(0))
         nc.scalar.dma_start(out=bias_row[0:1, COL_A], in_=alpha_bias.unsqueeze(0))
         w_plain = keep.tile([P, GATES], BF16)
-        nc.scalar.dma_start(out=w_plain[:, COL_IOG], in_=weight_hh)
+        nc.sync.dma_start(out=w_plain[:, COL_IOG], in_=weight_hh)
         nc.scalar.dma_start(out=w_plain[:, COL_A], in_=alpha_weight_hh)
+        h_rest = keep.tile([P, ROW_TILES - GROUP, H], BF16)
+        nc.sync.dma_start(out=h_rest[:], in_=h_rows[:, GROUP:ROW_TILES, :])
+        c_rest = keep.tile([P, ROW_TILES - GROUP, H], BF16)
+        nc.scalar.dma_start(out=c_rest[:], in_=c_rows[:, GROUP:ROW_TILES, :])
+
+        def tiles_of(first, rest, lo, hi):
+            if hi <= GROUP:
+                return first[:, lo:hi, :]
+            return rest[:, lo - GROUP : hi - GROUP, :]
+
         x_sb = []
         for s in range(X_LOADS):
             x_part = keep.tile([P, TILES_PER_LOAD, I], BF16, name="x_part%d" % s)
@@ -133,8 +143,12 @@ def tile_multiinputlstmcell_pa_s_kernel(
             if not 0 <= j < ROW_TILES:
                 return
             hc_ps = turn_ps.tile([P, 2, P], BF16, tag="turn")
-            nc.tensor.transpose(out=hc_ps[:, 0, :], in_=h_sb[:, j, :], identity=ident_bf16[:])
-            nc.tensor.transpose(out=hc_ps[:, 1, :], in_=c_sb[:, j, :], identity=ident_bf16[:])
+            for which, (first, rest) in enumerate(((h_first, h_rest), (c_first, c_rest))):
+                nc.tensor.transpose(
+                    out=hc_ps[:, which, :],
+                    in_=tiles_of(first, rest, j, j + 1).rearrange("p o h -> p (o h)"),
+                    identity=ident_bf16[:],
+                )
             hc_t[j] = work.tile([P, 2, P], BF16, name="hc_t")
             nc.scalar.copy(out=hc_t[j][:], in_=hc_ps[:])
 
@@ -197,11 +211,11 @@ def tile_multiinputlstmcell_pa_s_kernel(
             nc.scalar.activation(out=of_tile[:, COL_G], in_=pre[:, COL_G], func=ACT.Tanh)
 
         turn_hc(0)
-        turn_hc(1)
         spread_biases()
+        turn_hc(1)
         for j in range(ROW_TILES + 3):
-            turn_hc(j + 2)
             plain_products(j)
+            turn_hc(j + 2)
             turn_x(j - 2)
             quantise(j - 3)
 
@@ -214,7 +228,7 @@ def tile_multiinputlstmcell_pa_s_kernel(
             mx_products(j + 2)
 
         for g in range(GROUPS):
-            c_in = c_sb[:, g * GROUP : (g + 1) * GROUP, :]
+            c_in = tiles_of(c_first, c_rest, g * GROUP, (g + 1) * GROUP)
             i_minus_a = work.tile([P, GROUP, H], F32)
             nc.vector.tensor_tensor(
                 out=i_minus_a[:], in0=gates[g][:, :, COL_I], in1=gates[g][:, :, COL_A], op=ALU.subtract
@@ -228,7 +242,8 @@ def tile_multiinputlstmcell_pa_s_kernel(
             nc.vector.tensor_tensor(out=c_1[g][:], in0=w_i[g][:], in1=g_minus_c[g][:], op=ALU.mult)
         for g in range(GROUPS):
             tiles = slice(g * GROUP, (g + 1) * GROUP)
-            nc.vector.tensor_tensor(out=c_1[g][:], in0=c_1[g][:], in1=c_sb[:, tiles, :], op=ALU.add)
+            c_in = tiles_of(c_first, c_rest, g * GROUP, (g + 1) * GROUP)
+            nc.vector.tensor_tensor(out=c_1[g][:], in0=c_1[g][:], in1=c_in, op=ALU.add)
             nc.sync.dma_start(out=c1_rows[:, tiles, :], in_=c_1[g][:])
             tanh_c1[g] = work.tile([P, GROUP, H], F32, name="tanh_c1")
             nc.scalar.activation(out=tanh_c1[g][:], in_=c_1[g][:], func=ACT.Tanh)

@@ -23,6 +23,7 @@ X_LOADS = 2
 TILES_PER_LOAD = ROW_TILES // X_LOADS
 GROUP = 2
 GROUPS = ROW_TILES // GROUP
+SUM_BANKS = 4
 
 FLOPS = 2 * B * I * GATES + 2 * B * H * GATES
 
@@ -60,8 +61,7 @@ def tile_multiinputlstmcell_pa_s_kernel(
         keep = ctx.enter_context(tc.tile_pool(name="keep", bufs=1))
         work = ctx.enter_context(tc.tile_pool(name="work", bufs=ROW_TILES))
         turn_ps = ctx.enter_context(tc.psum_pool(name="turn_ps", bufs=4))
-        plain_ps = ctx.enter_context(tc.psum_pool(name="plain_ps", bufs=2))
-        mx_ps = ctx.enter_context(tc.psum_pool(name="mx_ps", bufs=2))
+        sums_ps = ctx.enter_context(tc.psum_pool(name="sums_ps", bufs=SUM_BANKS))
         ctx.enter_context(tc.manual_schedule())
 
         bias_row = keep.tile([P, GATES], BF16)
@@ -135,7 +135,7 @@ def tile_multiinputlstmcell_pa_s_kernel(
         tanh_c1 = {}
 
         def spread_biases():
-            bias_ps = plain_ps.tile([P, GATES], F32, tag="plain")
+            bias_ps = sums_ps.tile([P, GATES], F32, tag="sums")
             nc.tensor.matmul(out=bias_ps[:], lhsT=ones[:], rhs=bias_row[:], start=True, stop=True)
             nc.vector.tensor_copy(out=bias_all[:], in_=bias_ps[:])
 
@@ -155,7 +155,7 @@ def tile_multiinputlstmcell_pa_s_kernel(
         def plain_products(j):
             if not 0 <= j < ROW_TILES:
                 return
-            plain = plain_ps.tile([P, GATES], F32, tag="plain")
+            plain = sums_ps.tile([P, GATES], F32, tag="sums")
             nc.tensor.matmul(
                 out=plain[:, COL_IOG], lhsT=hc_t[j][:, 0, :], rhs=w_plain[:, COL_IOG], start=True, stop=True
             )
@@ -192,7 +192,7 @@ def tile_multiinputlstmcell_pa_s_kernel(
             if not 0 <= j < ROW_TILES:
                 return
             rows = slice(j * P, (j + 1) * P)
-            acc[j] = mx_ps.tile([P, GATES], F32, name="acc")
+            acc[j] = sums_ps.tile([P, GATES], F32, name="acc", tag="sums")
             nc.tensor.matmul_mx(
                 out=acc[j][:],
                 lhsT=x_codes[:, rows].bitcast(FP8X4),
@@ -221,11 +221,11 @@ def tile_multiinputlstmcell_pa_s_kernel(
 
         for g in range(GROUPS):
             gates[g] = keep.tile([P, GROUP, GATES], F32, name="gates%d" % g)
-        mx_products(0)
-        mx_products(1)
+        for j in range(SUM_BANKS):
+            mx_products(j)
         for j in range(ROW_TILES):
             four_gates(j)
-            mx_products(j + 2)
+            mx_products(j + SUM_BANKS)
 
         for g in range(GROUPS):
             c_in = tiles_of(c_first, c_rest, g * GROUP, (g + 1) * GROUP)

@@ -97,6 +97,14 @@ def tile_multiinputlstmcell_pa_s_kernel(
                 return first[:, lo:hi, :]
             return rest[:, lo - GROUP : hi - GROUP, :]
 
+        def scale_rows(scales, cols):
+            for q in range(4):
+                nc.sync.dma_start(
+                    out=w_scales[32 * q : 32 * q + 4, cols].bitcast(I32),
+                    in_=scales[0, 4 * q : 4 * q + 4, :].bitcast(I32),
+                )
+
+        scale_rows(weight_ih_scales, COL_IOG)
         x_sb = []
         for s in range(X_LOADS):
             x_part = keep.tile([P, TILES_PER_LOAD, I], BF16, name="x_part%d" % s)
@@ -111,12 +119,7 @@ def tile_multiinputlstmcell_pa_s_kernel(
         nc.sync.dma_start(
             out=w_words[:, 0 : 2 * H].bitcast(I32), in_=alpha_weight_ih_words[0].bitcast(I32)
         )
-        for scales, cols in ((weight_ih_scales, COL_IOG), (alpha_weight_ih_scales, COL_A)):
-            for q in range(4):
-                nc.sync.dma_start(
-                    out=w_scales[32 * q : 32 * q + 4, cols].bitcast(I32),
-                    in_=scales[0, 4 * q : 4 * q + 4, :].bitcast(I32),
-                )
+        scale_rows(alpha_weight_ih_scales, COL_A)
 
         warm_out = keep.tile([P, 1], F32)
         nc.scalar.activation(out=warm_out[:], in_=warm_in[:], func=ACT.Sigmoid)

@@ -64,6 +64,17 @@ def tile_multiinputlstmcell_pa_s_kernel(
         sums_ps = ctx.enter_context(tc.psum_pool(name="sums_ps", bufs=SUM_BANKS))
         ctx.enter_context(tc.manual_schedule())
 
+        x_sb = []
+
+        def load_x(s):
+            x_part = keep.tile([P, TILES_PER_LOAD, I], BF16, name="x_part%d" % s)
+            nc.gpsimd.dma_start(
+                out=x_part[:], in_=x_rows[:, s * TILES_PER_LOAD : (s + 1) * TILES_PER_LOAD, :]
+            )
+            x_sb.append(x_part)
+
+        load_x(0)
+
         bias_row = keep.tile([P, GATES], BF16)
         nc.vector.memset(bias_row[:], 0.0)
         ident_f32 = keep.tile([P, P], F32)
@@ -78,40 +89,16 @@ def tile_multiinputlstmcell_pa_s_kernel(
         ident_bf16 = keep.tile([P, P], BF16)
         nc.vector.tensor_copy(out=ident_bf16[:], in_=ident_f32[:])
 
-        h_first = keep.tile([P, GROUP, H], BF16)
-        nc.sync.dma_start(out=h_first[:], in_=h_rows[:, 0:GROUP, :])
-        c_first = keep.tile([P, GROUP, H], BF16)
-        nc.scalar.dma_start(out=c_first[:], in_=c_rows[:, 0:GROUP, :])
+        load_x(1)
+        h_sb = keep.tile([P, ROW_TILES, H], BF16)
+        nc.sync.dma_start(out=h_sb[:], in_=h_rows)
+        c_sb = keep.tile([P, ROW_TILES, H], BF16)
+        nc.scalar.dma_start(out=c_sb[:], in_=c_rows)
         nc.scalar.dma_start(out=bias_row[0:1, COL_IOG], in_=bias.unsqueeze(0))
         nc.scalar.dma_start(out=bias_row[0:1, COL_A], in_=alpha_bias.unsqueeze(0))
         w_plain = keep.tile([P, GATES], BF16)
         nc.sync.dma_start(out=w_plain[:, COL_IOG], in_=weight_hh)
         nc.scalar.dma_start(out=w_plain[:, COL_A], in_=alpha_weight_hh)
-        h_rest = keep.tile([P, ROW_TILES - GROUP, H], BF16)
-        nc.sync.dma_start(out=h_rest[:], in_=h_rows[:, GROUP:ROW_TILES, :])
-        c_rest = keep.tile([P, ROW_TILES - GROUP, H], BF16)
-        nc.scalar.dma_start(out=c_rest[:], in_=c_rows[:, GROUP:ROW_TILES, :])
-
-        def tiles_of(first, rest, lo, hi):
-            if hi <= GROUP:
-                return first[:, lo:hi, :]
-            return rest[:, lo - GROUP : hi - GROUP, :]
-
-        def scale_rows(scales, cols):
-            for q in range(4):
-                nc.sync.dma_start(
-                    out=w_scales[32 * q : 32 * q + 4, cols].bitcast(I32),
-                    in_=scales[0, 4 * q : 4 * q + 4, :].bitcast(I32),
-                )
-
-        scale_rows(weight_ih_scales, COL_IOG)
-        x_sb = []
-        for s in range(X_LOADS):
-            x_part = keep.tile([P, TILES_PER_LOAD, I], BF16, name="x_part%d" % s)
-            nc.sync.dma_start(
-                out=x_part[:], in_=x_rows[:, s * TILES_PER_LOAD : (s + 1) * TILES_PER_LOAD, :]
-            )
-            x_sb.append(x_part)
         w_words = keep.tile([P, 2 * GATES], U8, align_bytes=64)
         nc.sync.dma_start(
             out=w_words[:, 2 * H : 2 * GATES].bitcast(I32), in_=weight_ih_words[0].bitcast(I32)
@@ -119,7 +106,12 @@ def tile_multiinputlstmcell_pa_s_kernel(
         nc.sync.dma_start(
             out=w_words[:, 0 : 2 * H].bitcast(I32), in_=alpha_weight_ih_words[0].bitcast(I32)
         )
-        scale_rows(alpha_weight_ih_scales, COL_A)
+        for scales, cols in ((weight_ih_scales, COL_IOG), (alpha_weight_ih_scales, COL_A)):
+            for q in range(4):
+                nc.sync.dma_start(
+                    out=w_scales[32 * q : 32 * q + 4, cols].bitcast(I32),
+                    in_=scales[0, 4 * q : 4 * q + 4, :].bitcast(I32),
+                )
 
         warm_out = keep.tile([P, 1], F32)
         nc.scalar.activation(out=warm_out[:], in_=warm_in[:], func=ACT.Sigmoid)
@@ -146,12 +138,8 @@ def tile_multiinputlstmcell_pa_s_kernel(
             if not 0 <= j < ROW_TILES:
                 return
             hc_ps = turn_ps.tile([P, 2, P], BF16, tag="turn")
-            for which, (first, rest) in enumerate(((h_first, h_rest), (c_first, c_rest))):
-                nc.tensor.transpose(
-                    out=hc_ps[:, which, :],
-                    in_=tiles_of(first, rest, j, j + 1).rearrange("p o h -> p (o h)"),
-                    identity=ident_bf16[:],
-                )
+            for which, rows_sb in enumerate((h_sb, c_sb)):
+                nc.tensor.transpose(out=hc_ps[:, which, :], in_=rows_sb[:, j, :], identity=ident_bf16[:])
             hc_t[j] = work.tile([P, 2, P], BF16, name="hc_t")
             nc.scalar.copy(out=hc_t[j][:], in_=hc_ps[:])
 
@@ -231,7 +219,7 @@ def tile_multiinputlstmcell_pa_s_kernel(
             mx_products(j + SUM_BANKS)
 
         for g in range(GROUPS):
-            c_in = tiles_of(c_first, c_rest, g * GROUP, (g + 1) * GROUP)
+            c_in = c_sb[:, g * GROUP : (g + 1) * GROUP, :]
             i_minus_a = work.tile([P, GROUP, H], F32)
             nc.vector.tensor_tensor(
                 out=i_minus_a[:], in0=gates[g][:, :, COL_I], in1=gates[g][:, :, COL_A], op=ALU.subtract
@@ -245,7 +233,7 @@ def tile_multiinputlstmcell_pa_s_kernel(
             nc.vector.tensor_tensor(out=c_1[g][:], in0=w_i[g][:], in1=g_minus_c[g][:], op=ALU.mult)
         for g in range(GROUPS):
             tiles = slice(g * GROUP, (g + 1) * GROUP)
-            c_in = tiles_of(c_first, c_rest, g * GROUP, (g + 1) * GROUP)
+            c_in = c_sb[:, g * GROUP : (g + 1) * GROUP, :]
             nc.vector.tensor_tensor(out=c_1[g][:], in0=c_1[g][:], in1=c_in, op=ALU.add)
             nc.sync.dma_start(out=c1_rows[:, tiles, :], in_=c_1[g][:])
             tanh_c1[g] = work.tile([P, GROUP, H], F32, name="tanh_c1")

@@ -24,6 +24,7 @@ TILES_PER_LOAD = ROW_TILES // X_LOADS
 GROUP = 2
 GROUPS = ROW_TILES // GROUP
 SUM_BANKS = 4
+WARM_COLUMNS = 256
 
 FLOPS = 2 * B * I * GATES + 2 * B * H * GATES
 
@@ -72,6 +73,11 @@ def tile_multiinputlstmcell_pa_s_kernel(
                 out=x_part[:], in_=x_rows[:, s * TILES_PER_LOAD : (s + 1) * TILES_PER_LOAD, :]
             )
             x_sb.append(x_part)
+
+        zeros = keep.tile([P, WARM_COLUMNS], F32)
+        nc.gpsimd.memset(zeros[:], 0.0)
+        warm_ps = turn_ps.tile([P, WARM_COLUMNS], F32, tag="turn")
+        nc.tensor.matmul(out=warm_ps[:], lhsT=zeros[:, 0:P], rhs=zeros[:], start=True, stop=True)
 
         load_x(0)
 

@@ -97,14 +97,25 @@ def tile_multiinputlstmcell_pa_s_kernel(
 
         load_x(1)
         h_sb = keep.tile([P, ROW_TILES, H], BF16)
-        nc.sync.dma_start(out=h_sb[:], in_=h_rows)
+        nc.sync.dma_start(out=h_sb[:, 0:GROUP, :], in_=h_rows[:, 0:GROUP, :])
         c_sb = keep.tile([P, ROW_TILES, H], BF16)
-        nc.scalar.dma_start(out=c_sb[:], in_=c_rows)
+        nc.scalar.dma_start(out=c_sb[:, 0:GROUP, :], in_=c_rows[:, 0:GROUP, :])
         nc.scalar.dma_start(out=bias_row[0:1, COL_IOG], in_=bias.unsqueeze(0))
         nc.scalar.dma_start(out=bias_row[0:1, COL_A], in_=alpha_bias.unsqueeze(0))
         w_plain = keep.tile([P, GATES], BF16)
         nc.sync.dma_start(out=w_plain[:, COL_IOG], in_=weight_hh)
         nc.scalar.dma_start(out=w_plain[:, COL_A], in_=alpha_weight_hh)
+        nc.sync.dma_start(out=h_sb[:, GROUP:ROW_TILES, :], in_=h_rows[:, GROUP:ROW_TILES, :])
+        nc.scalar.dma_start(out=c_sb[:, GROUP:ROW_TILES, :], in_=c_rows[:, GROUP:ROW_TILES, :])
+
+        def scale_rows(scales, cols, quarters):
+            for q in quarters:
+                nc.sync.dma_start(
+                    out=w_scales[32 * q : 32 * q + 4, cols].bitcast(I32),
+                    in_=scales[0, 4 * q : 4 * q + 4, :].bitcast(I32),
+                )
+
+        scale_rows(weight_ih_scales, COL_IOG, (0, 1))
         w_words = keep.tile([P, 2 * GATES], U8, align_bytes=64)
         nc.sync.dma_start(
             out=w_words[:, 2 * H : 2 * GATES].bitcast(I32), in_=weight_ih_words[0].bitcast(I32)
@@ -112,12 +123,8 @@ def tile_multiinputlstmcell_pa_s_kernel(
         nc.sync.dma_start(
             out=w_words[:, 0 : 2 * H].bitcast(I32), in_=alpha_weight_ih_words[0].bitcast(I32)
         )
-        for scales, cols in ((weight_ih_scales, COL_IOG), (alpha_weight_ih_scales, COL_A)):
-            for q in range(4):
-                nc.sync.dma_start(
-                    out=w_scales[32 * q : 32 * q + 4, cols].bitcast(I32),
-                    in_=scales[0, 4 * q : 4 * q + 4, :].bitcast(I32),
-                )
+        scale_rows(weight_ih_scales, COL_IOG, (2, 3))
+        scale_rows(alpha_weight_ih_scales, COL_A, (0, 1, 2, 3))
 
         warm_out = keep.tile([P, 1], F32)
         nc.scalar.activation(out=warm_out[:], in_=warm_in[:], func=ACT.Sigmoid)

@@ -82,7 +82,9 @@ def tile_multiinputlstmcell_pa_s_kernel(
         load_x(0)
 
         bias_row = keep.tile([P, GATES], BF16)
-        nc.vector.memset(bias_row[:], 0.0)
+        nc.vector.memset(bias_row[:].bitcast(I32), 0)
+        warm_in = keep.tile([P, 1], F32)
+        nc.vector.memset(warm_in[:], 0.0)
         ident_f32 = keep.tile([P, P], F32)
         nc.vector.memset(ident_f32[:], 0.0)
         make_identity(nc, ident_f32[:], nomemset=True)
@@ -90,8 +92,6 @@ def tile_multiinputlstmcell_pa_s_kernel(
         nc.vector.memset(w_scales[:].bitcast(I32), 0)
         ones = keep.tile([P, P], BF16)
         nc.vector.memset(ones[:], 1.0)
-        warm_in = keep.tile([P, 1], F32)
-        nc.vector.memset(warm_in[:], 0.0)
         ident_bf16 = keep.tile([P, P], BF16)
         nc.vector.tensor_copy(out=ident_bf16[:], in_=ident_f32[:])
 
@@ -100,13 +100,15 @@ def tile_multiinputlstmcell_pa_s_kernel(
         nc.sync.dma_start(out=h_sb[:, 0:GROUP, :], in_=h_rows[:, 0:GROUP, :])
         c_sb = keep.tile([P, ROW_TILES, H], BF16)
         nc.scalar.dma_start(out=c_sb[:, 0:GROUP, :], in_=c_rows[:, 0:GROUP, :])
-        nc.scalar.dma_start(out=bias_row[0:1, COL_IOG], in_=bias.unsqueeze(0))
-        nc.scalar.dma_start(out=bias_row[0:1, COL_A], in_=alpha_bias.unsqueeze(0))
+        warm_out = keep.tile([P, 1], F32)
+        nc.scalar.activation(out=warm_out[:], in_=warm_in[:], func=ACT.Sigmoid)
         w_plain = keep.tile([P, GATES], BF16)
         nc.sync.dma_start(out=w_plain[:, COL_IOG], in_=weight_hh)
-        nc.scalar.dma_start(out=w_plain[:, COL_A], in_=alpha_weight_hh)
+        nc.sync.dma_start(out=w_plain[:, COL_A], in_=alpha_weight_hh)
+        nc.sync.dma_start(out=bias_row[0:1, COL_IOG], in_=bias.unsqueeze(0))
+        nc.sync.dma_start(out=bias_row[0:1, COL_A], in_=alpha_bias.unsqueeze(0))
         nc.sync.dma_start(out=h_sb[:, GROUP:ROW_TILES, :], in_=h_rows[:, GROUP:ROW_TILES, :])
-        nc.scalar.dma_start(out=c_sb[:, GROUP:ROW_TILES, :], in_=c_rows[:, GROUP:ROW_TILES, :])
+        nc.sync.dma_start(out=c_sb[:, GROUP:ROW_TILES, :], in_=c_rows[:, GROUP:ROW_TILES, :])
 
         def scale_rows(scales, cols, quarters):
             for q in quarters:
@@ -125,9 +127,6 @@ def tile_multiinputlstmcell_pa_s_kernel(
         )
         scale_rows(weight_ih_scales, COL_IOG, (2, 3))
         scale_rows(alpha_weight_ih_scales, COL_A, (0, 1, 2, 3))
-
-        warm_out = keep.tile([P, 1], F32)
-        nc.scalar.activation(out=warm_out[:], in_=warm_in[:], func=ACT.Sigmoid)
 
         bias_all = keep.tile([P, GATES], F32)
         x_codes = keep.tile([P, B], U32, align_bytes=64)

@@ -76,6 +76,9 @@ def tile_multiinputlstmcell_pa_s_kernel(
 
         zeros = keep.tile([P, WARM_COLUMNS], F32)
         nc.gpsimd.memset(zeros[:], 0.0)
+        ident_f32 = keep.tile([P, P], F32)
+        nc.vector.memset(ident_f32[:], 0.0)
+        make_identity(nc, ident_f32[:], nomemset=True)
         warm_ps = turn_ps.tile([P, WARM_COLUMNS], F32, tag="turn")
         nc.tensor.matmul(out=warm_ps[:], lhsT=zeros[:, 0:P], rhs=zeros[:], start=True, stop=True)
 
@@ -85,9 +88,6 @@ def tile_multiinputlstmcell_pa_s_kernel(
         nc.vector.memset(bias_row[:].bitcast(I32), 0)
         warm_in = keep.tile([P, 1], F32)
         nc.vector.memset(warm_in[:], 0.0)
-        ident_f32 = keep.tile([P, P], F32)
-        nc.vector.memset(ident_f32[:], 0.0)
-        make_identity(nc, ident_f32[:], nomemset=True)
         w_scales = keep.tile([P, GATES], U8, align_bytes=64)
         nc.vector.memset(w_scales[:].bitcast(I32), 0)
         ones = keep.tile([P, P], BF16)
@@ -214,8 +214,8 @@ def tile_multiinputlstmcell_pa_s_kernel(
             nc.scalar.activation(out=of_tile[:, COL_G], in_=pre[:, COL_G], func=ACT.Tanh)
 
         turn_hc(0)
-        spread_biases()
         turn_hc(1)
+        spread_biases()
         for j in range(ROW_TILES + 3):
             plain_products(j)
             turn_hc(j + 2)

@@ -74,22 +74,22 @@ def tile_multiinputlstmcell_pa_s_kernel(
             )
             x_sb.append(x_part)
 
-        zeros = keep.tile([P, WARM_COLUMNS], F32)
-        nc.gpsimd.memset(zeros[:], 0.0)
+        bias_row = keep.tile([P, GATES], BF16)
+        nc.gpsimd.memset(bias_row[:].bitcast(F32), 0.0)
         ident_f32 = keep.tile([P, P], F32)
         nc.vector.memset(ident_f32[:], 0.0)
         make_identity(nc, ident_f32[:], nomemset=True)
-        warm_ps = turn_ps.tile([P, WARM_COLUMNS], F32, tag="turn")
-        nc.tensor.matmul(out=warm_ps[:], lhsT=zeros[:, 0:P], rhs=zeros[:], start=True, stop=True)
 
         load_x(0)
 
-        bias_row = keep.tile([P, GATES], BF16)
-        nc.vector.memset(bias_row[:].bitcast(I32), 0)
         warm_in = keep.tile([P, 1], F32)
         nc.vector.memset(warm_in[:], 0.0)
         w_scales = keep.tile([P, GATES], U8, align_bytes=64)
         nc.vector.memset(w_scales[:].bitcast(I32), 0)
+        zeros = keep.tile([P, WARM_COLUMNS], F32)
+        nc.vector.memset(zeros[:], 0.0)
+        warm_ps = turn_ps.tile([P, WARM_COLUMNS], F32, tag="turn")
+        nc.tensor.matmul(out=warm_ps[:], lhsT=zeros[:, 0:P], rhs=zeros[:], start=True, stop=True)
         ones = keep.tile([P, P], BF16)
         nc.vector.memset(ones[:], 1.0)
         ident_bf16 = keep.tile([P, P], BF16)
@@ -104,9 +104,9 @@ def tile_multiinputlstmcell_pa_s_kernel(
         nc.scalar.activation(out=warm_out[:], in_=warm_in[:], func=ACT.Sigmoid)
         w_plain = keep.tile([P, GATES], BF16)
         nc.sync.dma_start(out=w_plain[:, COL_IOG], in_=weight_hh)
-        nc.sync.dma_start(out=w_plain[:, COL_A], in_=alpha_weight_hh)
         nc.sync.dma_start(out=bias_row[0:1, COL_IOG], in_=bias.unsqueeze(0))
         nc.sync.dma_start(out=bias_row[0:1, COL_A], in_=alpha_bias.unsqueeze(0))
+        nc.sync.dma_start(out=w_plain[:, COL_A], in_=alpha_weight_hh)
         nc.sync.dma_start(out=h_sb[:, GROUP:ROW_TILES, :], in_=h_rows[:, GROUP:ROW_TILES, :])
         nc.sync.dma_start(out=c_sb[:, GROUP:ROW_TILES, :], in_=c_rows[:, GROUP:ROW_TILES, :])
 
@@ -142,9 +142,10 @@ def tile_multiinputlstmcell_pa_s_kernel(
         tanh_c1 = {}
 
         def spread_biases():
-            bias_ps = sums_ps.tile([P, GATES], F32, tag="sums")
-            nc.tensor.matmul(out=bias_ps[:], lhsT=ones[:], rhs=bias_row[:], start=True, stop=True)
-            nc.vector.tensor_copy(out=bias_all[:], in_=bias_ps[:])
+            for cols, copy in ((slice(0, GATES // 2), nc.vector.tensor_copy), (slice(GATES // 2, GATES), nc.scalar.copy)):
+                bias_ps = sums_ps.tile([P, GATES // 2], F32, name="bias_ps", tag="sums")
+                nc.tensor.matmul(out=bias_ps[:], lhsT=ones[:], rhs=bias_row[:, cols], start=True, stop=True)
+                copy(out=bias_all[:, cols], in_=bias_ps[:])
 
         def turn_hc(j):
             if not 0 <= j < ROW_TILES:
@@ -168,27 +169,25 @@ def tile_multiinputlstmcell_pa_s_kernel(
             plain_sb[j] = work.tile([P, GATES], F32, name="plain_sb")
             nc.vector.tensor_tensor(out=plain_sb[j][:], in0=plain[:], in1=bias_all[:], op=ALU.add)
 
-        def turn_x(j):
-            if not 0 <= j < ROW_TILES:
-                return
-            x_words = x_sb[j // TILES_PER_LOAD][:, j % TILES_PER_LOAD, :].bitcast(F32)
-            x_ps = turn_ps.tile([P, 2, P], F32, tag="turn")
-            for u in range(2):
-                nc.tensor.transpose(out=x_ps[:, u, :], in_=x_words[:, u : I // 2 : 2], identity=ident_f32[:])
-            grouped[j] = work.tile([P, P, 4], BF16, name="grouped", align_bytes=64)
+        def turn_x(g):
+            x_ps = turn_ps.tile([P, GROUP, 2, P], F32, tag="turn")
+            for a in range(GROUP):
+                j = g * GROUP + a
+                x_words = x_sb[j // TILES_PER_LOAD][:, j % TILES_PER_LOAD, :].bitcast(F32)
+                for u in range(2):
+                    nc.tensor.transpose(out=x_ps[:, a, u, :], in_=x_words[:, u : I // 2 : 2], identity=ident_f32[:])
+            grouped[g] = work.tile([P, GROUP * P, 4], BF16, name="grouped", align_bytes=64)
             nc.scalar.copy(
-                out=grouped[j][:].rearrange("p b t -> p (b t)").bitcast(F32).rearrange("p (b u) -> p b u", u=2),
-                in_=x_ps[:].rearrange("p u b -> p b u"),
+                out=grouped[g][:].rearrange("p b t -> p (b t)").bitcast(F32).rearrange("p (a b u) -> p a b u", a=GROUP, u=2),
+                in_=x_ps[:].rearrange("p a u b -> p a b u"),
             )
 
-        def quantise(j):
-            if not 0 <= j < ROW_TILES:
-                return
-            rows = slice(j * P, (j + 1) * P)
+        def quantise(g):
+            rows = slice(g * GROUP * P, (g + 1) * GROUP * P)
             nc.vector.quantize_mx(
                 out=x_codes[:, rows].bitcast(FP8X4),
                 scales=x_scales[:, rows],
-                in_=grouped[j][:].rearrange("p b t -> p (b t)"),
+                in_=grouped[g][:].rearrange("p b t -> p (b t)"),
             )
 
         def mx_products(j):
@@ -216,11 +215,22 @@ def tile_multiinputlstmcell_pa_s_kernel(
         turn_hc(0)
         turn_hc(1)
         spread_biases()
-        for j in range(ROW_TILES + 3):
-            plain_products(j)
-            turn_hc(j + 2)
-            turn_x(j - 2)
-            quantise(j - 3)
+        plain_products(0)
+        turn_hc(2)
+        plain_products(1)
+        turn_hc(3)
+        plain_products(2)
+        turn_hc(4)
+        plain_products(3)
+        turn_hc(5)
+        turn_x(0)
+        plain_products(4)
+        plain_products(5)
+        turn_x(1)
+        quantise(0)
+        turn_x(2)
+        quantise(1)
+        quantise(2)
 
         for g in range(GROUPS):
             gates[g] = keep.tile([P, GROUP, GATES], F32, name="gates%d" % g)

@@ -19,6 +19,7 @@ I = 512
 H = 128
 ROW_TILES = B // P
 GATES = 4 * H
+ADDED = 3 * H
 X_LOADS = 2
 TILES_PER_LOAD = ROW_TILES // X_LOADS
 GROUP = 2
@@ -51,7 +52,9 @@ def tile_multiinputlstmcell_pa_s_kernel(
     COL_O = slice(2 * H, 3 * H)
     COL_G = slice(3 * H, 4 * H)
     COL_IOG = slice(1 * H, 4 * H)
-    COL_SIGMOID = slice(0, 3 * H)
+    COL_AI = slice(0 * H, 2 * H)
+    ADD_AI = slice(0, 2 * H)
+    ADD_G = slice(2 * H, 3 * H)
     x_rows = input_.rearrange("(p j) k -> p j k", j=ROW_TILES)
     h_rows = h_0.rearrange("(p j) h -> p j h", j=ROW_TILES)
     c_rows = c_input.rearrange("(p j) o h -> p j (o h)", j=ROW_TILES)
@@ -128,7 +131,11 @@ def tile_multiinputlstmcell_pa_s_kernel(
         scale_rows(weight_ih_scales, COL_IOG, (2, 3))
         scale_rows(alpha_weight_ih_scales, COL_A, (0, 1, 2, 3))
 
-        bias_all = keep.tile([P, GATES], F32)
+        bias_all = keep.tile([P, ADDED], F32)
+        bias_o = keep.tile([P, 1], F32)
+        o_t = keep.tile([P, B], F32)
+        o_sb = keep.tile([P, ROW_TILES, H], F32)
+        o_ps = {}
         x_codes = keep.tile([P, B], U32, align_bytes=64)
         x_scales = keep.tile([P, B], U8, align_bytes=64)
         hc_t = {}
@@ -142,10 +149,48 @@ def tile_multiinputlstmcell_pa_s_kernel(
         tanh_c1 = {}
 
         def spread_biases():
-            for cols, copy in ((slice(0, GATES // 2), nc.vector.tensor_copy), (slice(GATES // 2, GATES), nc.scalar.copy)):
-                bias_ps = sums_ps.tile([P, GATES // 2], F32, name="bias_ps", tag="sums")
+            for to, cols, copy in ((ADD_AI, COL_AI, nc.vector.tensor_copy), (ADD_G, COL_G, nc.scalar.copy)):
+                bias_ps = sums_ps.tile([P, to.stop - to.start], F32, name="bias_ps", tag="sums")
                 nc.tensor.matmul(out=bias_ps[:], lhsT=ones[:], rhs=bias_row[:, cols], start=True, stop=True)
-                copy(out=bias_all[:, cols], in_=bias_ps[:])
+                copy(out=bias_all[:, to], in_=bias_ps[:])
+
+        def turn_bias_o():
+            bias_ps = turn_ps.tile([P, P], BF16, name="bias_o_ps", tag="turn")
+            nc.tensor.transpose(out=bias_ps[:], in_=bias_row[:, COL_O], identity=ident_bf16[:])
+            nc.vector.tensor_copy(out=bias_o[:], in_=bias_ps[:, 0:1])
+
+        def mx_o(first, tiles):
+            rows = slice(first * P, (first + tiles) * P)
+            o_ps["mx", first] = turn_ps.tile([P, tiles * P], F32, name="o_mx", tag="turn")
+            nc.tensor.matmul_mx(
+                out=o_ps["mx", first][:],
+                lhsT=w_words[:, 2 * COL_O.start : 2 * COL_O.stop].bitcast(FP4X4),
+                lhsT_scale=w_scales[:, COL_O],
+                rhs=x_codes[:, rows].bitcast(FP8X4),
+                rhs_scale=x_scales[:, rows],
+                start=True,
+                stop=True,
+            )
+
+        def copy_o(first, tiles):
+            nc.scalar.activation(
+                out=o_t[:, first * P : (first + tiles) * P],
+                in_=o_ps["mx", first][:],
+                func=ACT.Identity,
+                bias=bias_o[:],
+            )
+
+        def sum_o(first, tiles):
+            o_ps["sum", first] = turn_ps.tile([P, tiles, H], F32, name="o_sum", tag="turn")
+            for j in range(first, first + tiles):
+                out = o_ps["sum", first][:, j - first, :]
+                nc.tensor.matmul(out=out, lhsT=hc_t[j][:, 0, :], rhs=w_plain[:, COL_O], start=True, stop=False)
+                nc.tensor.matmul(
+                    out=out, lhsT=o_t[:, j * P : (j + 1) * P], rhs=ident_f32[:], start=False, stop=True, is_transpose=True
+                )
+
+        def sigmoid_o(first, tiles):
+            nc.scalar.activation(out=o_sb[:, first : first + tiles, :], in_=o_ps["sum", first][:], func=ACT.Sigmoid)
 
         def turn_hc(j):
             if not 0 <= j < ROW_TILES:
@@ -159,14 +204,16 @@ def tile_multiinputlstmcell_pa_s_kernel(
         def plain_products(j):
             if not 0 <= j < ROW_TILES:
                 return
-            plain = sums_ps.tile([P, GATES], F32, tag="sums")
-            nc.tensor.matmul(
-                out=plain[:, COL_IOG], lhsT=hc_t[j][:, 0, :], rhs=w_plain[:, COL_IOG], start=True, stop=True
-            )
-            nc.tensor.matmul(
-                out=plain[:, COL_A], lhsT=hc_t[j][:, 1, :], rhs=w_plain[:, COL_A], start=True, stop=True
-            )
-            plain_sb[j] = work.tile([P, GATES], F32, name="plain_sb")
+            plain = sums_ps.tile([P, ADDED], F32, tag="sums")
+            for n, (which, cols) in enumerate(((1, COL_A), (0, COL_I), (0, COL_G))):
+                nc.tensor.matmul(
+                    out=plain[:, n * H : (n + 1) * H],
+                    lhsT=hc_t[j][:, which, :],
+                    rhs=w_plain[:, cols],
+                    start=True,
+                    stop=True,
+                )
+            plain_sb[j] = work.tile([P, ADDED], F32, name="plain_sb")
             nc.vector.tensor_tensor(out=plain_sb[j][:], in0=plain[:], in1=bias_all[:], op=ALU.add)
 
         def turn_x(g):
@@ -194,23 +241,65 @@ def tile_multiinputlstmcell_pa_s_kernel(
             if not 0 <= j < ROW_TILES:
                 return
             rows = slice(j * P, (j + 1) * P)
-            acc[j] = sums_ps.tile([P, GATES], F32, name="acc", tag="sums")
-            nc.tensor.matmul_mx(
-                out=acc[j][:],
-                lhsT=x_codes[:, rows].bitcast(FP8X4),
-                lhsT_scale=x_scales[:, rows],
-                rhs=w_words[:].bitcast(FP4X4),
-                rhs_scale=w_scales[:],
-                start=True,
-                stop=True,
-            )
+            acc[j] = sums_ps.tile([P, ADDED], F32, name="acc", tag="sums")
+            for to, cols in ((ADD_AI, COL_AI), (ADD_G, COL_G)):
+                nc.tensor.matmul_mx(
+                    out=acc[j][:, to],
+                    lhsT=x_codes[:, rows].bitcast(FP8X4),
+                    lhsT_scale=x_scales[:, rows],
+                    rhs=w_words[:, 2 * cols.start : 2 * cols.stop].bitcast(FP4X4),
+                    rhs_scale=w_scales[:, cols],
+                    start=True,
+                    stop=True,
+                )
 
         def four_gates(j):
-            pre = work.tile([P, GATES], F32)
+            pre = work.tile([P, ADDED], F32)
             nc.vector.tensor_tensor(out=pre[:], in0=acc[j][:], in1=plain_sb[j][:], op=ALU.add)
             of_tile = gates[j // GROUP][:, j % GROUP, :]
-            nc.scalar.activation(out=of_tile[:, COL_SIGMOID], in_=pre[:, COL_SIGMOID], func=ACT.Sigmoid)
-            nc.scalar.activation(out=of_tile[:, COL_G], in_=pre[:, COL_G], func=ACT.Tanh)
+            nc.scalar.activation(out=of_tile[:, ADD_AI], in_=pre[:, ADD_AI], func=ACT.Sigmoid)
+            nc.scalar.activation(out=of_tile[:, ADD_G], in_=pre[:, ADD_G], func=ACT.Tanh)
+
+        for g in range(GROUPS):
+            gates[g] = keep.tile([P, GROUP, ADDED], F32, name="gates%d" % g)
+        i_minus_a = {}
+
+        def tiles_of(g):
+            return slice(g * GROUP, (g + 1) * GROUP)
+
+        def i_minus_alpha(g):
+            i_minus_a[g] = work.tile([P, GROUP, H], F32, name="i_minus_a")
+            nc.vector.tensor_tensor(
+                out=i_minus_a[g][:], in0=gates[g][:, :, H : 2 * H], in1=gates[g][:, :, 0:H], op=ALU.subtract
+            )
+
+        def weight(g):
+            w_i[g] = work.tile([P, GROUP, H], F32, name="w_i")
+            nc.scalar.activation(out=w_i[g][:], in_=i_minus_a[g][:], func=ACT.Sigmoid)
+
+        def difference(g):
+            g_minus_c[g] = work.tile([P, GROUP, H], F32, name="g_minus_c")
+            nc.vector.tensor_tensor(
+                out=g_minus_c[g][:], in0=gates[g][:, :, ADD_G], in1=c_sb[:, tiles_of(g), :], op=ALU.subtract
+            )
+
+        def weighted(g):
+            c_1[g] = work.tile([P, GROUP, H], F32, name="c_1")
+            nc.vector.tensor_tensor(out=c_1[g][:], in0=w_i[g][:], in1=g_minus_c[g][:], op=ALU.mult)
+
+        def add_c(g):
+            nc.vector.tensor_tensor(out=c_1[g][:], in0=c_1[g][:], in1=c_sb[:, tiles_of(g), :], op=ALU.add)
+            nc.sync.dma_start(out=c1_rows[:, tiles_of(g), :], in_=c_1[g][:])
+
+        def tanh_of_c1(g):
+            tanh_c1[g] = work.tile([P, GROUP, H], F32, name="tanh_c1")
+            nc.scalar.activation(out=tanh_c1[g][:], in_=c_1[g][:], func=ACT.Tanh)
+
+        def output(g):
+            h_1 = work.tile([P, GROUP, H], F32)
+            nc.vector.tensor_tensor(out=h_1[:], in0=o_sb[:, tiles_of(g), :], in1=tanh_c1[g][:], op=ALU.mult)
+            nc.sync.dma_start(out=h1_rows[:, tiles_of(g), :], in_=h_1[:])
+
 
         turn_hc(0)
         turn_hc(1)
@@ -229,39 +318,47 @@ def tile_multiinputlstmcell_pa_s_kernel(
         turn_x(1)
         quantise(0)
         turn_x(2)
+        mx_products(0)
+        mx_products(1)
         quantise(1)
+        four_gates(0)
+        turn_bias_o()
         quantise(2)
-
-        for g in range(GROUPS):
-            gates[g] = keep.tile([P, GROUP, GATES], F32, name="gates%d" % g)
-        for j in range(SUM_BANKS):
-            mx_products(j)
-        for j in range(ROW_TILES):
-            four_gates(j)
-            mx_products(j + SUM_BANKS)
-
-        for g in range(GROUPS):
-            c_in = c_sb[:, g * GROUP : (g + 1) * GROUP, :]
-            i_minus_a = work.tile([P, GROUP, H], F32)
-            nc.vector.tensor_tensor(
-                out=i_minus_a[:], in0=gates[g][:, :, COL_I], in1=gates[g][:, :, COL_A], op=ALU.subtract
-            )
-            w_i[g] = work.tile([P, GROUP, H], F32, name="w_i")
-            nc.scalar.activation(out=w_i[g][:], in_=i_minus_a[:], func=ACT.Sigmoid)
-            g_minus_c[g] = work.tile([P, GROUP, H], F32, name="g_minus_c")
-            nc.vector.tensor_tensor(out=g_minus_c[g][:], in0=gates[g][:, :, COL_G], in1=c_in, op=ALU.subtract)
-        for g in range(GROUPS):
-            c_1[g] = work.tile([P, GROUP, H], F32, name="c_1")
-            nc.vector.tensor_tensor(out=c_1[g][:], in0=w_i[g][:], in1=g_minus_c[g][:], op=ALU.mult)
-        for g in range(GROUPS):
-            tiles = slice(g * GROUP, (g + 1) * GROUP)
-            c_in = c_sb[:, g * GROUP : (g + 1) * GROUP, :]
-            nc.vector.tensor_tensor(out=c_1[g][:], in0=c_1[g][:], in1=c_in, op=ALU.add)
-            nc.sync.dma_start(out=c1_rows[:, tiles, :], in_=c_1[g][:])
-            tanh_c1[g] = work.tile([P, GROUP, H], F32, name="tanh_c1")
-            nc.scalar.activation(out=tanh_c1[g][:], in_=c_1[g][:], func=ACT.Tanh)
-        for g in range(GROUPS):
-            tiles = slice(g * GROUP, (g + 1) * GROUP)
-            h_1 = work.tile([P, GROUP, H], F32)
-            nc.vector.tensor_tensor(out=h_1[:], in0=gates[g][:, :, COL_O], in1=tanh_c1[g][:], op=ALU.mult)
-            nc.sync.dma_start(out=h1_rows[:, tiles, :], in_=h_1[:])
+        mx_products(2)
+        mx_products(3)
+        four_gates(1)
+        mx_o(0, 4)
+        mx_products(4)
+        four_gates(2)
+        mx_products(5)
+        four_gates(3)
+        mx_o(4, 2)
+        four_gates(4)
+        copy_o(0, 4)
+        four_gates(5)
+        i_minus_alpha(0)
+        weight(0)
+        difference(0)
+        sum_o(0, 4)
+        i_minus_alpha(1)
+        weight(1)
+        difference(1)
+        copy_o(4, 2)
+        i_minus_alpha(2)
+        weight(2)
+        difference(2)
+        sum_o(4, 2)
+        weighted(0)
+        weighted(1)
+        weighted(2)
+        sigmoid_o(0, 4)
+        add_c(0)
+        tanh_of_c1(0)
+        sigmoid_o(4, 2)
+        add_c(1)
+        tanh_of_c1(1)
+        add_c(2)
+        tanh_of_c1(2)
+        output(0)
+        output(1)
+        output(2)

@@ -18,14 +18,13 @@ B = 768
 I = 512
 H = 128
 ROW_TILES = B // P
+PAIR = 2
+PAIRS = ROW_TILES // PAIR
 GATES = 4 * H
-ADDED = 3 * H
-X_LOADS = 2
-TILES_PER_LOAD = ROW_TILES // X_LOADS
-GROUP = 2
-GROUPS = ROW_TILES // GROUP
-SUM_BANKS = 4
+BLOCKS = ((0, 4), (4, 2))
+X_LOADS = ((0, 4), (4, 2))
 WARM_COLUMNS = 256
+WARM_MATMULS = 1
 
 FLOPS = 2 * B * I * GATES + 2 * B * H * GATES
 
@@ -51,10 +50,8 @@ def tile_multiinputlstmcell_pa_s_kernel(
     COL_I = slice(1 * H, 2 * H)
     COL_O = slice(2 * H, 3 * H)
     COL_G = slice(3 * H, 4 * H)
-    COL_IOG = slice(1 * H, 4 * H)
     COL_AI = slice(0 * H, 2 * H)
-    ADD_AI = slice(0, 2 * H)
-    ADD_G = slice(2 * H, 3 * H)
+    COL_IOG = slice(1 * H, 4 * H)
     x_rows = input_.rearrange("(p j) k -> p j k", j=ROW_TILES)
     h_rows = h_0.rearrange("(p j) h -> p j h", j=ROW_TILES)
     c_rows = c_input.rearrange("(p j) o h -> p j (o h)", j=ROW_TILES)
@@ -63,46 +60,39 @@ def tile_multiinputlstmcell_pa_s_kernel(
 
     with ExitStack() as ctx:
         keep = ctx.enter_context(tc.tile_pool(name="keep", bufs=1))
-        work = ctx.enter_context(tc.tile_pool(name="work", bufs=ROW_TILES))
-        turn_ps = ctx.enter_context(tc.psum_pool(name="turn_ps", bufs=4))
-        sums_ps = ctx.enter_context(tc.psum_pool(name="sums_ps", bufs=SUM_BANKS))
+        banks = ctx.enter_context(tc.psum_pool(name="banks", bufs=8))
         ctx.enter_context(tc.manual_schedule())
-
-        x_sb = []
-
-        def load_x(s):
-            x_part = keep.tile([P, TILES_PER_LOAD, I], BF16, name="x_part%d" % s)
-            nc.gpsimd.dma_start(
-                out=x_part[:], in_=x_rows[:, s * TILES_PER_LOAD : (s + 1) * TILES_PER_LOAD, :]
-            )
-            x_sb.append(x_part)
 
         bias_row = keep.tile([P, GATES], BF16)
         nc.gpsimd.memset(bias_row[:].bitcast(F32), 0.0)
         ident_f32 = keep.tile([P, P], F32)
         nc.vector.memset(ident_f32[:], 0.0)
         make_identity(nc, ident_f32[:], nomemset=True)
-
-        load_x(0)
-
         warm_in = keep.tile([P, 1], F32)
         nc.vector.memset(warm_in[:], 0.0)
         w_scales = keep.tile([P, GATES], U8, align_bytes=64)
         nc.vector.memset(w_scales[:].bitcast(I32), 0)
         zeros = keep.tile([P, WARM_COLUMNS], F32)
         nc.vector.memset(zeros[:], 0.0)
-        warm_ps = turn_ps.tile([P, WARM_COLUMNS], F32, tag="turn")
-        nc.tensor.matmul(out=warm_ps[:], lhsT=zeros[:, 0:P], rhs=zeros[:], start=True, stop=True)
         ones = keep.tile([P, P], BF16)
         nc.vector.memset(ones[:], 1.0)
         ident_bf16 = keep.tile([P, P], BF16)
         nc.vector.tensor_copy(out=ident_bf16[:], in_=ident_f32[:])
 
-        load_x(1)
+        warm_ps = banks.tile([P, WARM_COLUMNS], F32, name="warm_ps", tag="bank")
+        for w in range(WARM_MATMULS):
+            nc.tensor.matmul(out=warm_ps[:], lhsT=zeros[:, 0:P], rhs=zeros[:], start=True, stop=True)
+
+        x_sb = []
+        for s, (first, tiles) in enumerate(X_LOADS):
+            x_part = keep.tile([P, tiles, I], BF16, name="x_part%d" % s)
+            nc.gpsimd.dma_start(out=x_part[:], in_=x_rows[:, first : first + tiles, :])
+            for a in range(tiles):
+                x_sb.append(x_part[:, a, :])
         h_sb = keep.tile([P, ROW_TILES, H], BF16)
-        nc.sync.dma_start(out=h_sb[:, 0:GROUP, :], in_=h_rows[:, 0:GROUP, :])
+        nc.sync.dma_start(out=h_sb[:, 0:PAIR, :], in_=h_rows[:, 0:PAIR, :])
         c_sb = keep.tile([P, ROW_TILES, H], BF16)
-        nc.scalar.dma_start(out=c_sb[:, 0:GROUP, :], in_=c_rows[:, 0:GROUP, :])
+        nc.scalar.dma_start(out=c_sb[:, 0:PAIR, :], in_=c_rows[:, 0:PAIR, :])
         warm_out = keep.tile([P, 1], F32)
         nc.scalar.activation(out=warm_out[:], in_=warm_in[:], func=ACT.Sigmoid)
         w_plain = keep.tile([P, GATES], BF16)
@@ -110,8 +100,8 @@ def tile_multiinputlstmcell_pa_s_kernel(
         nc.sync.dma_start(out=bias_row[0:1, COL_IOG], in_=bias.unsqueeze(0))
         nc.sync.dma_start(out=bias_row[0:1, COL_A], in_=alpha_bias.unsqueeze(0))
         nc.sync.dma_start(out=w_plain[:, COL_A], in_=alpha_weight_hh)
-        nc.sync.dma_start(out=h_sb[:, GROUP:ROW_TILES, :], in_=h_rows[:, GROUP:ROW_TILES, :])
-        nc.sync.dma_start(out=c_sb[:, GROUP:ROW_TILES, :], in_=c_rows[:, GROUP:ROW_TILES, :])
+        nc.sync.dma_start(out=h_sb[:, PAIR:ROW_TILES, :], in_=h_rows[:, PAIR:ROW_TILES, :])
+        nc.sync.dma_start(out=c_sb[:, PAIR:ROW_TILES, :], in_=c_rows[:, PAIR:ROW_TILES, :])
 
         def scale_rows(scales, cols, quarters):
             for q in quarters:
@@ -131,234 +121,241 @@ def tile_multiinputlstmcell_pa_s_kernel(
         scale_rows(weight_ih_scales, COL_IOG, (2, 3))
         scale_rows(alpha_weight_ih_scales, COL_A, (0, 1, 2, 3))
 
-        bias_all = keep.tile([P, ADDED], F32)
-        bias_o = keep.tile([P, 1], F32)
-        o_t = keep.tile([P, B], F32)
-        o_sb = keep.tile([P, ROW_TILES, H], F32)
-        o_ps = {}
+        bias_ai = keep.tile([P, PAIR, 2 * H], F32)
+        bias_t = keep.tile([P, 2], F32)
         x_codes = keep.tile([P, B], U32, align_bytes=64)
         x_scales = keep.tile([P, B], U8, align_bytes=64)
-        hc_t = {}
-        plain_sb = {}
-        grouped = {}
-        acc = {}
-        gates = {}
-        g_minus_c = {}
-        w_i = {}
-        c_1 = {}
-        tanh_c1 = {}
+        og_t = [keep.tile([P, B], F32, name="og_t%d" % n) for n in range(2)]
+        og = [keep.tile([P, ROW_TILES, H], F32, name="og%d" % n) for n in range(2)]
+        t = {}
+
+        def tiles_of(p):
+            return slice(p * PAIR, (p + 1) * PAIR)
 
         def spread_biases():
-            for to, cols, copy in ((ADD_AI, COL_AI, nc.vector.tensor_copy), (ADD_G, COL_G, nc.scalar.copy)):
-                bias_ps = sums_ps.tile([P, to.stop - to.start], F32, name="bias_ps", tag="sums")
-                nc.tensor.matmul(out=bias_ps[:], lhsT=ones[:], rhs=bias_row[:, cols], start=True, stop=True)
-                copy(out=bias_all[:, to], in_=bias_ps[:])
+            for a, copy in enumerate((nc.vector.tensor_copy, nc.scalar.copy)):
+                bias_ps = banks.tile([P, 2 * H], F32, name="bias_ps", tag="bank")
+                nc.tensor.matmul(out=bias_ps[:], lhsT=ones[:], rhs=bias_row[:, COL_AI], start=True, stop=True)
+                copy(out=bias_ai[:, a, :], in_=bias_ps[:])
 
-        def turn_bias_o():
-            bias_ps = turn_ps.tile([P, P], BF16, name="bias_o_ps", tag="turn")
-            nc.tensor.transpose(out=bias_ps[:], in_=bias_row[:, COL_O], identity=ident_bf16[:])
-            nc.vector.tensor_copy(out=bias_o[:], in_=bias_ps[:, 0:1])
+        def turn_biases():
+            bias_ps = banks.tile([P, 2, P], BF16, name="bias_t_ps", tag="bank")
+            for n, cols in enumerate((COL_O, COL_G)):
+                nc.tensor.transpose(out=bias_ps[:, n, :], in_=bias_row[:, cols], identity=ident_bf16[:])
+            nc.vector.tensor_copy(out=bias_t[:], in_=bias_ps[:, :, 0])
 
-        def mx_o(first, tiles):
+        def turn_hc(p, copy):
+            hc_ps = banks.tile([P, PAIR, 2, P], BF16, name="hc_ps", tag="bank")
+            for a in range(PAIR):
+                for which, rows_sb in enumerate((h_sb, c_sb)):
+                    nc.tensor.transpose(
+                        out=hc_ps[:, a, which, :], in_=rows_sb[:, p * PAIR + a, :], identity=ident_bf16[:]
+                    )
+            t["hc", p] = keep.tile([P, PAIR, 2, P], BF16, name="hc%d" % p)
+            copy(out=t["hc", p][:], in_=hc_ps[:])
+
+        def plain_ai(p):
+            plain_ps = banks.tile([P, PAIR, 2 * H], F32, name="plain_ps", tag="bank")
+            for a in range(PAIR):
+                for which, cols in ((0, COL_I), (1, COL_A)):
+                    nc.tensor.matmul(
+                        out=plain_ps[:, a, cols],
+                        lhsT=t["hc", p][:, a, which, :],
+                        rhs=w_plain[:, cols],
+                        start=True,
+                        stop=True,
+                    )
+            t["plain", p] = keep.tile([P, PAIR, 2 * H], F32, name="plain%d" % p)
+            nc.vector.tensor_tensor(out=t["plain", p][:], in0=plain_ps[:], in1=bias_ai[:], op=ALU.add)
+
+        def turn_x(p, copy):
+            x_ps = banks.tile([P, PAIR, 2, P], F32, name="x_ps", tag="bank")
+            for a in range(PAIR):
+                x_words = x_sb[p * PAIR + a].bitcast(F32)
+                for u in range(2):
+                    nc.tensor.transpose(out=x_ps[:, a, u, :], in_=x_words[:, u : I // 2 : 2], identity=ident_f32[:])
+            t["grouped", p] = keep.tile([P, PAIR * P, 4], BF16, name="grouped%d" % p, align_bytes=64)
+            copy(
+                out=t["grouped", p][:]
+                .rearrange("p b t -> p (b t)")
+                .bitcast(F32)
+                .rearrange("p (a b u) -> p a b u", a=PAIR, u=2),
+                in_=x_ps[:].rearrange("p a u b -> p a b u"),
+            )
+
+        def quantise(p):
+            rows = slice(p * PAIR * P, (p + 1) * PAIR * P)
+            nc.vector.quantize_mx(
+                out=x_codes[:, rows].bitcast(FP8X4),
+                scales=x_scales[:, rows],
+                in_=t["grouped", p][:].rearrange("p b t -> p (b t)"),
+            )
+
+        def mx_ai(p):
+            t["ai_ps", p] = banks.tile([P, PAIR, 2 * H], F32, name="ai_ps", tag="bank")
+            for a in range(PAIR):
+                rows = slice((p * PAIR + a) * P, (p * PAIR + a + 1) * P)
+                nc.tensor.matmul_mx(
+                    out=t["ai_ps", p][:, a, :],
+                    lhsT=x_codes[:, rows].bitcast(FP8X4),
+                    lhsT_scale=x_scales[:, rows],
+                    rhs=w_words[:, 0 : 4 * H].bitcast(FP4X4),
+                    rhs_scale=w_scales[:, COL_AI],
+                    start=True,
+                    stop=True,
+                )
+
+        def gates_ai(p):
+            pre = keep.tile([P, PAIR, 2 * H], F32, name="pre%d" % p)
+            nc.vector.tensor_tensor(out=pre[:], in0=t["ai_ps", p][:], in1=t["plain", p][:], op=ALU.add)
+            t["ai", p] = keep.tile([P, PAIR, 2 * H], F32, name="ai%d" % p)
+            nc.scalar.activation(out=t["ai", p][:], in_=pre[:], func=ACT.Sigmoid)
+
+        def mx_og(n, block):
+            first, tiles = BLOCKS[block]
+            cols = (COL_O, COL_G)[n]
             rows = slice(first * P, (first + tiles) * P)
-            o_ps["mx", first] = turn_ps.tile([P, tiles * P], F32, name="o_mx", tag="turn")
+            t["og_ps", n, block] = banks.tile([P, tiles * P], F32, name="og_ps", tag="bank")
             nc.tensor.matmul_mx(
-                out=o_ps["mx", first][:],
-                lhsT=w_words[:, 2 * COL_O.start : 2 * COL_O.stop].bitcast(FP4X4),
-                lhsT_scale=w_scales[:, COL_O],
+                out=t["og_ps", n, block][:],
+                lhsT=w_words[:, 2 * cols.start : 2 * cols.stop].bitcast(FP4X4),
+                lhsT_scale=w_scales[:, cols],
                 rhs=x_codes[:, rows].bitcast(FP8X4),
                 rhs_scale=x_scales[:, rows],
                 start=True,
                 stop=True,
             )
 
-        def copy_o(first, tiles):
+        def copy_og_vector(n, block):
+            first, tiles = BLOCKS[block]
+            nc.vector.tensor_scalar(
+                out=og_t[n][:, first * P : (first + tiles) * P],
+                in0=t["og_ps", n, block][:],
+                scalar1=bias_t[:, n : n + 1],
+                scalar2=None,
+                op0=ALU.add,
+            )
+
+        def copy_og_scalar(n, block):
+            first, tiles = BLOCKS[block]
             nc.scalar.activation(
-                out=o_t[:, first * P : (first + tiles) * P],
-                in_=o_ps["mx", first][:],
+                out=og_t[n][:, first * P : (first + tiles) * P],
+                in_=t["og_ps", n, block][:],
                 func=ACT.Identity,
-                bias=bias_o[:],
+                bias=bias_t[:, n : n + 1],
             )
 
-        def sum_o(first, tiles):
-            o_ps["sum", first] = turn_ps.tile([P, tiles, H], F32, name="o_sum", tag="turn")
+        def sum_og(n, block):
+            first, tiles = BLOCKS[block]
+            cols = (COL_O, COL_G)[n]
+            t["og_sum", n, block] = banks.tile([P, tiles, H], F32, name="og_sum", tag="bank")
             for j in range(first, first + tiles):
-                out = o_ps["sum", first][:, j - first, :]
-                nc.tensor.matmul(out=out, lhsT=hc_t[j][:, 0, :], rhs=w_plain[:, COL_O], start=True, stop=False)
+                out = t["og_sum", n, block][:, j - first, :]
                 nc.tensor.matmul(
-                    out=out, lhsT=o_t[:, j * P : (j + 1) * P], rhs=ident_f32[:], start=False, stop=True, is_transpose=True
+                    out=out, lhsT=t["hc", j // PAIR][:, j % PAIR, 0, :], rhs=w_plain[:, cols], start=True, stop=False
                 )
-
-        def sigmoid_o(first, tiles):
-            nc.scalar.activation(out=o_sb[:, first : first + tiles, :], in_=o_ps["sum", first][:], func=ACT.Sigmoid)
-
-        def turn_hc(j):
-            if not 0 <= j < ROW_TILES:
-                return
-            hc_ps = turn_ps.tile([P, 2, P], BF16, tag="turn")
-            for which, rows_sb in enumerate((h_sb, c_sb)):
-                nc.tensor.transpose(out=hc_ps[:, which, :], in_=rows_sb[:, j, :], identity=ident_bf16[:])
-            hc_t[j] = work.tile([P, 2, P], BF16, name="hc_t")
-            nc.scalar.copy(out=hc_t[j][:], in_=hc_ps[:])
-
-        def plain_products(j):
-            if not 0 <= j < ROW_TILES:
-                return
-            plain = sums_ps.tile([P, ADDED], F32, tag="sums")
-            for n, (which, cols) in enumerate(((1, COL_A), (0, COL_I), (0, COL_G))):
                 nc.tensor.matmul(
-                    out=plain[:, n * H : (n + 1) * H],
-                    lhsT=hc_t[j][:, which, :],
-                    rhs=w_plain[:, cols],
-                    start=True,
+                    out=out,
+                    lhsT=og_t[n][:, j * P : (j + 1) * P],
+                    rhs=ident_f32[:],
+                    start=False,
                     stop=True,
-                )
-            plain_sb[j] = work.tile([P, ADDED], F32, name="plain_sb")
-            nc.vector.tensor_tensor(out=plain_sb[j][:], in0=plain[:], in1=bias_all[:], op=ALU.add)
-
-        def turn_x(g):
-            x_ps = turn_ps.tile([P, GROUP, 2, P], F32, tag="turn")
-            for a in range(GROUP):
-                j = g * GROUP + a
-                x_words = x_sb[j // TILES_PER_LOAD][:, j % TILES_PER_LOAD, :].bitcast(F32)
-                for u in range(2):
-                    nc.tensor.transpose(out=x_ps[:, a, u, :], in_=x_words[:, u : I // 2 : 2], identity=ident_f32[:])
-            grouped[g] = work.tile([P, GROUP * P, 4], BF16, name="grouped", align_bytes=64)
-            nc.scalar.copy(
-                out=grouped[g][:].rearrange("p b t -> p (b t)").bitcast(F32).rearrange("p (a b u) -> p a b u", a=GROUP, u=2),
-                in_=x_ps[:].rearrange("p a u b -> p a b u"),
-            )
-
-        def quantise(g):
-            rows = slice(g * GROUP * P, (g + 1) * GROUP * P)
-            nc.vector.quantize_mx(
-                out=x_codes[:, rows].bitcast(FP8X4),
-                scales=x_scales[:, rows],
-                in_=grouped[g][:].rearrange("p b t -> p (b t)"),
-            )
-
-        def mx_products(j):
-            if not 0 <= j < ROW_TILES:
-                return
-            rows = slice(j * P, (j + 1) * P)
-            acc[j] = sums_ps.tile([P, ADDED], F32, name="acc", tag="sums")
-            for to, cols in ((ADD_AI, COL_AI), (ADD_G, COL_G)):
-                nc.tensor.matmul_mx(
-                    out=acc[j][:, to],
-                    lhsT=x_codes[:, rows].bitcast(FP8X4),
-                    lhsT_scale=x_scales[:, rows],
-                    rhs=w_words[:, 2 * cols.start : 2 * cols.stop].bitcast(FP4X4),
-                    rhs_scale=w_scales[:, cols],
-                    start=True,
-                    stop=True,
+                    is_transpose=True,
                 )
 
-        def four_gates(j):
-            pre = work.tile([P, ADDED], F32)
-            nc.vector.tensor_tensor(out=pre[:], in0=acc[j][:], in1=plain_sb[j][:], op=ALU.add)
-            of_tile = gates[j // GROUP][:, j % GROUP, :]
-            nc.scalar.activation(out=of_tile[:, ADD_AI], in_=pre[:, ADD_AI], func=ACT.Sigmoid)
-            nc.scalar.activation(out=of_tile[:, ADD_G], in_=pre[:, ADD_G], func=ACT.Tanh)
-
-        for g in range(GROUPS):
-            gates[g] = keep.tile([P, GROUP, ADDED], F32, name="gates%d" % g)
-        i_minus_a = {}
-
-        def tiles_of(g):
-            return slice(g * GROUP, (g + 1) * GROUP)
-
-        def i_minus_alpha(g):
-            i_minus_a[g] = work.tile([P, GROUP, H], F32, name="i_minus_a")
-            nc.vector.tensor_tensor(
-                out=i_minus_a[g][:], in0=gates[g][:, :, H : 2 * H], in1=gates[g][:, :, 0:H], op=ALU.subtract
+        def gate_og(n, block):
+            first, tiles = BLOCKS[block]
+            nc.scalar.activation(
+                out=og[n][:, first : first + tiles, :],
+                in_=t["og_sum", n, block][:],
+                func=(ACT.Sigmoid, ACT.Tanh)[n],
             )
 
-        def weight(g):
-            w_i[g] = work.tile([P, GROUP, H], F32, name="w_i")
-            nc.scalar.activation(out=w_i[g][:], in_=i_minus_a[g][:], func=ACT.Sigmoid)
+        def cell_tile(p, name):
+            t[name, p] = keep.tile([P, PAIR, H], F32, name="%s%d" % (name, p))
+            return t[name, p][:]
 
-        def difference(g):
-            g_minus_c[g] = work.tile([P, GROUP, H], F32, name="g_minus_c")
+        def i_minus_alpha(p):
             nc.vector.tensor_tensor(
-                out=g_minus_c[g][:], in0=gates[g][:, :, ADD_G], in1=c_sb[:, tiles_of(g), :], op=ALU.subtract
+                out=cell_tile(p, "d"), in0=t["ai", p][:, :, COL_I], in1=t["ai", p][:, :, COL_A], op=ALU.subtract
             )
 
-        def weighted(g):
-            c_1[g] = work.tile([P, GROUP, H], F32, name="c_1")
-            nc.vector.tensor_tensor(out=c_1[g][:], in0=w_i[g][:], in1=g_minus_c[g][:], op=ALU.mult)
+        def weight(p):
+            nc.scalar.activation(out=cell_tile(p, "w"), in_=t["d", p][:], func=ACT.Sigmoid)
 
-        def add_c(g):
-            nc.vector.tensor_tensor(out=c_1[g][:], in0=c_1[g][:], in1=c_sb[:, tiles_of(g), :], op=ALU.add)
-            nc.sync.dma_start(out=c1_rows[:, tiles_of(g), :], in_=c_1[g][:])
+        def g_minus_c(p):
+            nc.vector.tensor_tensor(
+                out=cell_tile(p, "e"), in0=og[1][:, tiles_of(p), :], in1=c_sb[:, tiles_of(p), :], op=ALU.subtract
+            )
 
-        def tanh_of_c1(g):
-            tanh_c1[g] = work.tile([P, GROUP, H], F32, name="tanh_c1")
-            nc.scalar.activation(out=tanh_c1[g][:], in_=c_1[g][:], func=ACT.Tanh)
+        def weighted(p):
+            nc.vector.tensor_tensor(out=cell_tile(p, "m"), in0=t["w", p][:], in1=t["e", p][:], op=ALU.mult)
 
-        def output(g):
-            h_1 = work.tile([P, GROUP, H], F32)
-            nc.vector.tensor_tensor(out=h_1[:], in0=o_sb[:, tiles_of(g), :], in1=tanh_c1[g][:], op=ALU.mult)
-            nc.sync.dma_start(out=h1_rows[:, tiles_of(g), :], in_=h_1[:])
+        def add_c(p):
+            nc.vector.tensor_tensor(out=cell_tile(p, "c1"), in0=t["m", p][:], in1=c_sb[:, tiles_of(p), :], op=ALU.add)
+            nc.sync.dma_start(out=c1_rows[:, tiles_of(p), :], in_=t["c1", p][:])
 
+        def tanh_c1(p):
+            nc.scalar.activation(out=cell_tile(p, "t"), in_=t["c1", p][:], func=ACT.Tanh)
 
-        turn_hc(0)
-        turn_hc(1)
+        def output(p):
+            nc.vector.tensor_tensor(out=cell_tile(p, "h1"), in0=og[0][:, tiles_of(p), :], in1=t["t", p][:], op=ALU.mult)
+            nc.sync.dma_start(out=h1_rows[:, tiles_of(p), :], in_=t["h1", p][:])
+
+        turn_hc(0, nc.scalar.copy)
         spread_biases()
-        plain_products(0)
-        turn_hc(2)
-        plain_products(1)
-        turn_hc(3)
-        plain_products(2)
-        turn_hc(4)
-        plain_products(3)
-        turn_hc(5)
-        turn_x(0)
-        plain_products(4)
-        plain_products(5)
-        turn_x(1)
+        turn_hc(1, nc.scalar.copy)
+        turn_hc(2, nc.scalar.copy)
+        plain_ai(0)
+        plain_ai(1)
+        turn_x(0, nc.scalar.copy)
+        turn_biases()
+        turn_x(1, nc.scalar.copy)
         quantise(0)
-        turn_x(2)
-        mx_products(0)
-        mx_products(1)
+        plain_ai(2)
+        turn_x(2, nc.scalar.copy)
         quantise(1)
-        four_gates(0)
-        turn_bias_o()
+        mx_ai(0)
+        mx_og(1, 0)
+        gates_ai(0)
+        mx_ai(1)
         quantise(2)
-        mx_products(2)
-        mx_products(3)
-        four_gates(1)
-        mx_o(0, 4)
-        mx_products(4)
-        four_gates(2)
-        mx_products(5)
-        four_gates(3)
-        mx_o(4, 2)
-        four_gates(4)
-        copy_o(0, 4)
-        four_gates(5)
+        mx_og(1, 1)
+        mx_og(0, 0)
+        copy_og_vector(1, 0)
+        mx_ai(2)
+        sum_og(1, 0)
+        copy_og_scalar(1, 1)
+        gates_ai(1)
         i_minus_alpha(0)
         weight(0)
-        difference(0)
-        sum_o(0, 4)
+        gate_og(1, 0)
+        copy_og_vector(0, 0)
+        gates_ai(2)
         i_minus_alpha(1)
-        weight(1)
-        difference(1)
-        copy_o(4, 2)
+        g_minus_c(0)
+        g_minus_c(1)
+        sum_og(1, 1)
+        gate_og(1, 1)
         i_minus_alpha(2)
-        weight(2)
-        difference(2)
-        sum_o(4, 2)
+        weight(1)
+        mx_og(0, 1)
+        sum_og(0, 0)
         weighted(0)
+        copy_og_scalar(0, 1)
+        g_minus_c(2)
         weighted(1)
-        weighted(2)
-        sigmoid_o(0, 4)
+        weight(2)
+        sum_og(0, 1)
         add_c(0)
-        tanh_of_c1(0)
-        sigmoid_o(4, 2)
+        gate_og(0, 0)
+        weighted(2)
         add_c(1)
-        tanh_of_c1(1)
+        tanh_c1(0)
+        gate_og(0, 1)
         add_c(2)
-        tanh_of_c1(2)
+        tanh_c1(1)
         output(0)
+        tanh_c1(2)
         output(1)
         output(2)

@@ -64,62 +64,72 @@ def tile_multiinputlstmcell_pa_s_kernel(
         ctx.enter_context(tc.manual_schedule())
 
         bias_row = keep.tile([P, GATES], BF16)
-        nc.gpsimd.memset(bias_row[:].bitcast(F32), 0.0)
         ident_f32 = keep.tile([P, P], F32)
+        warm_in = keep.tile([P, 1], F32)
+        w_scales = keep.tile([P, GATES], U8, align_bytes=64)
+        zeros = keep.tile([P, WARM_COLUMNS], F32)
+        ones = keep.tile([P, P], BF16)
+        ident_bf16 = keep.tile([P, P], BF16)
+        x_parts = [keep.tile([P, tiles, I], BF16, name="x_part%d" % s) for s, (first, tiles) in enumerate(X_LOADS)]
+        x_sb = [x_parts[s][:, a, :] for s, (first, tiles) in enumerate(X_LOADS) for a in range(tiles)]
+        h_sb = keep.tile([P, ROW_TILES, H], BF16)
+        c_sb = keep.tile([P, ROW_TILES, H], BF16)
+        w_plain = keep.tile([P, GATES], BF16)
+        w_words = keep.tile([P, 2 * GATES], U8, align_bytes=64)
+        warm_out = keep.tile([P, 1], F32)
+
+        def load_x(engine, s):
+            first, tiles = X_LOADS[s]
+            engine.dma_start(out=x_parts[s][:], in_=x_rows[:, first : first + tiles, :])
+
+        def load_scale(scales, cols, q):
+            nc.sync.dma_start(
+                out=w_scales[32 * q : 32 * q + 4, cols].bitcast(I32),
+                in_=scales[0, 4 * q : 4 * q + 4, :].bitcast(I32),
+            )
+
+        def load_table():
+            nc.scalar.activation(out=warm_out[:], in_=warm_in[:], func=ACT.Sigmoid)
+
+        def warm_up():
+            warm_ps = banks.tile([P, WARM_COLUMNS], F32, name="warm_ps", tag="bank")
+            for w in range(WARM_MATMULS):
+                nc.tensor.matmul(out=warm_ps[:], lhsT=zeros[:, 0:P], rhs=zeros[:], start=True, stop=True)
+
+        load_x(nc.gpsimd, 0)
         nc.vector.memset(ident_f32[:], 0.0)
         make_identity(nc, ident_f32[:], nomemset=True)
-        warm_in = keep.tile([P, 1], F32)
+        load_x(nc.gpsimd, 1)
+        nc.vector.memset(bias_row[:].bitcast(F32), 0.0)
         nc.vector.memset(warm_in[:], 0.0)
-        w_scales = keep.tile([P, GATES], U8, align_bytes=64)
-        nc.vector.memset(w_scales[:].bitcast(I32), 0)
-        zeros = keep.tile([P, WARM_COLUMNS], F32)
         nc.vector.memset(zeros[:], 0.0)
-        ones = keep.tile([P, P], BF16)
+        nc.vector.memset(w_scales[:].bitcast(I32), 0)
         nc.vector.memset(ones[:], 1.0)
-        ident_bf16 = keep.tile([P, P], BF16)
         nc.vector.tensor_copy(out=ident_bf16[:], in_=ident_f32[:])
-
-        warm_ps = banks.tile([P, WARM_COLUMNS], F32, name="warm_ps", tag="bank")
-        for w in range(WARM_MATMULS):
-            nc.tensor.matmul(out=warm_ps[:], lhsT=zeros[:, 0:P], rhs=zeros[:], start=True, stop=True)
-
-        x_sb = []
-        for s, (first, tiles) in enumerate(X_LOADS):
-            x_part = keep.tile([P, tiles, I], BF16, name="x_part%d" % s)
-            nc.gpsimd.dma_start(out=x_part[:], in_=x_rows[:, first : first + tiles, :])
-            for a in range(tiles):
-                x_sb.append(x_part[:, a, :])
-        h_sb = keep.tile([P, ROW_TILES, H], BF16)
+        warm_up()
         nc.sync.dma_start(out=h_sb[:, 0:PAIR, :], in_=h_rows[:, 0:PAIR, :])
-        c_sb = keep.tile([P, ROW_TILES, H], BF16)
         nc.scalar.dma_start(out=c_sb[:, 0:PAIR, :], in_=c_rows[:, 0:PAIR, :])
-        warm_out = keep.tile([P, 1], F32)
-        nc.scalar.activation(out=warm_out[:], in_=warm_in[:], func=ACT.Sigmoid)
-        w_plain = keep.tile([P, GATES], BF16)
-        nc.sync.dma_start(out=w_plain[:, COL_IOG], in_=weight_hh)
-        nc.sync.dma_start(out=bias_row[0:1, COL_IOG], in_=bias.unsqueeze(0))
-        nc.sync.dma_start(out=bias_row[0:1, COL_A], in_=alpha_bias.unsqueeze(0))
+        nc.scalar.dma_start(out=bias_row[0:1, COL_A], in_=alpha_bias.unsqueeze(0))
+        nc.scalar.dma_start(out=c_sb[:, PAIR:ROW_TILES, :], in_=c_rows[:, PAIR:ROW_TILES, :])
+        load_table()
         nc.sync.dma_start(out=w_plain[:, COL_A], in_=alpha_weight_hh)
+        nc.sync.dma_start(out=w_plain[:, COL_IOG], in_=weight_hh)
         nc.sync.dma_start(out=h_sb[:, PAIR:ROW_TILES, :], in_=h_rows[:, PAIR:ROW_TILES, :])
-        nc.sync.dma_start(out=c_sb[:, PAIR:ROW_TILES, :], in_=c_rows[:, PAIR:ROW_TILES, :])
-
-        def scale_rows(scales, cols, quarters):
-            for q in quarters:
-                nc.sync.dma_start(
-                    out=w_scales[32 * q : 32 * q + 4, cols].bitcast(I32),
-                    in_=scales[0, 4 * q : 4 * q + 4, :].bitcast(I32),
-                )
-
-        scale_rows(weight_ih_scales, COL_IOG, (0, 1))
-        w_words = keep.tile([P, 2 * GATES], U8, align_bytes=64)
+        nc.sync.dma_start(out=bias_row[0:1, COL_IOG], in_=bias.unsqueeze(0))
+        load_scale(alpha_weight_ih_scales, COL_A, 0)
+        load_scale(alpha_weight_ih_scales, COL_A, 1)
+        load_scale(alpha_weight_ih_scales, COL_A, 2)
+        load_scale(alpha_weight_ih_scales, COL_A, 3)
+        load_scale(weight_ih_scales, COL_IOG, 0)
+        load_scale(weight_ih_scales, COL_IOG, 1)
+        load_scale(weight_ih_scales, COL_IOG, 2)
+        load_scale(weight_ih_scales, COL_IOG, 3)
         nc.sync.dma_start(
             out=w_words[:, 2 * H : 2 * GATES].bitcast(I32), in_=weight_ih_words[0].bitcast(I32)
         )
         nc.sync.dma_start(
             out=w_words[:, 0 : 2 * H].bitcast(I32), in_=alpha_weight_ih_words[0].bitcast(I32)
         )
-        scale_rows(weight_ih_scales, COL_IOG, (2, 3))
-        scale_rows(alpha_weight_ih_scales, COL_A, (0, 1, 2, 3))
 
         bias_ai = keep.tile([P, PAIR, 2 * H], F32)
         bias_t = keep.tile([P, 2], F32)

@@ -309,18 +309,27 @@ def tile_multiinputlstmcell_pa_s_kernel(
             nc.scalar.activation(out=cell_tile(p, "t"), in_=t["c1", p][:], func=ACT.Tanh)
 
         def output(p):
-            nc.vector.tensor_tensor(out=cell_tile(p, "h1"), in0=og[0][:, tiles_of(p), :], in1=t["t", p][:], op=ALU.mult)
-            nc.sync.dma_start(out=h1_rows[:, tiles_of(p), :], in_=t["h1", p][:])
+            h_1 = cell_tile(p, "h1")
+            step = 1 if p == PAIRS - 1 else PAIR
+            for a in range(0, PAIR, step):
+                j = p * PAIR + a
+                nc.vector.tensor_tensor(
+                    out=h_1[:, a : a + step, :],
+                    in0=og[0][:, j : j + step, :],
+                    in1=t["t", p][:, a : a + step, :],
+                    op=ALU.mult,
+                )
+                nc.sync.dma_start(out=h1_rows[:, j : j + step, :], in_=h_1[:, a : a + step, :])
 
-        turn_hc(0, nc.scalar.copy)
+        turn_hc(0, nc.vector.tensor_copy)
         spread_biases()
-        turn_hc(1, nc.scalar.copy)
+        turn_hc(1, nc.vector.tensor_copy)
         turn_hc(2, nc.scalar.copy)
         plain_ai(0)
         plain_ai(1)
         turn_x(0, nc.scalar.copy)
-        turn_biases()
         turn_x(1, nc.scalar.copy)
+        turn_biases()
         quantise(0)
         plain_ai(2)
         turn_x(2, nc.scalar.copy)

@@ -120,16 +120,16 @@ def tile_multiinputlstmcell_pa_s_kernel(
         load_scale(alpha_weight_ih_scales, COL_A, 1)
         load_scale(alpha_weight_ih_scales, COL_A, 2)
         load_scale(alpha_weight_ih_scales, COL_A, 3)
-        load_scale(weight_ih_scales, COL_IOG, 0)
-        load_scale(weight_ih_scales, COL_IOG, 1)
-        load_scale(weight_ih_scales, COL_IOG, 2)
-        load_scale(weight_ih_scales, COL_IOG, 3)
         nc.sync.dma_start(
             out=w_words[:, 2 * H : 2 * GATES].bitcast(I32), in_=weight_ih_words[0].bitcast(I32)
         )
         nc.sync.dma_start(
             out=w_words[:, 0 : 2 * H].bitcast(I32), in_=alpha_weight_ih_words[0].bitcast(I32)
         )
+        load_scale(weight_ih_scales, COL_IOG, 0)
+        load_scale(weight_ih_scales, COL_IOG, 1)
+        load_scale(weight_ih_scales, COL_IOG, 2)
+        load_scale(weight_ih_scales, COL_IOG, 3)
 
         bias_ai = keep.tile([P, PAIR, 2 * H], F32)
         bias_t = keep.tile([P, 2], F32)
@@ -309,17 +309,8 @@ def tile_multiinputlstmcell_pa_s_kernel(
             nc.scalar.activation(out=cell_tile(p, "t"), in_=t["c1", p][:], func=ACT.Tanh)
 
         def output(p):
-            h_1 = cell_tile(p, "h1")
-            step = 1 if p == PAIRS - 1 else PAIR
-            for a in range(0, PAIR, step):
-                j = p * PAIR + a
-                nc.vector.tensor_tensor(
-                    out=h_1[:, a : a + step, :],
-                    in0=og[0][:, j : j + step, :],
-                    in1=t["t", p][:, a : a + step, :],
-                    op=ALU.mult,
-                )
-                nc.sync.dma_start(out=h1_rows[:, j : j + step, :], in_=h_1[:, a : a + step, :])
+            nc.vector.tensor_tensor(out=cell_tile(p, "h1"), in0=og[0][:, tiles_of(p), :], in1=t["t", p][:], op=ALU.mult)
+            nc.sync.dma_start(out=h1_rows[:, tiles_of(p), :], in_=t["h1", p][:])
 
         turn_hc(0, nc.vector.tensor_copy)
         spread_biases()

@@ -21,6 +21,7 @@ ROW_TILES = B // P
 PAIR = 2
 PAIRS = ROW_TILES // PAIR
 GATES = 4 * H
+ALPHA, GATE_I, GATE_O, GATE_G = range(4)
 BLOCKS = ((0, 4), (4, 2))
 X_LOADS = ((0, 4), (4, 2))
 WARM_COLUMNS = 256
@@ -68,7 +69,6 @@ def tile_multiinputlstmcell_pa_s_kernel(
         warm_in = keep.tile([P, 1], F32)
         w_scales = keep.tile([P, GATES], U8, align_bytes=64)
         zeros = keep.tile([P, WARM_COLUMNS], F32)
-        ones = keep.tile([P, P], BF16)
         ident_bf16 = keep.tile([P, P], BF16)
         x_parts = [keep.tile([P, tiles, I], BF16, name="x_part%d" % s) for s, (first, tiles) in enumerate(X_LOADS)]
         x_sb = [x_parts[s][:, a, :] for s, (first, tiles) in enumerate(X_LOADS) for a in range(tiles)]
@@ -93,90 +93,130 @@ def tile_multiinputlstmcell_pa_s_kernel(
 
         def warm_up():
             warm_ps = banks.tile([P, WARM_COLUMNS], F32, name="warm_ps", tag="bank")
-            for w in range(WARM_MATMULS):
-                nc.tensor.matmul(out=warm_ps[:], lhsT=zeros[:, 0:P], rhs=zeros[:], start=True, stop=True)
+            nc.tensor.matmul(out=warm_ps[:], lhsT=zeros[:, 0:P], rhs=zeros[:], start=True, stop=True)
 
-        load_x(nc.gpsimd, 0)
-        nc.vector.memset(ident_f32[:], 0.0)
-        make_identity(nc, ident_f32[:], nomemset=True)
-        load_x(nc.gpsimd, 1)
-        nc.vector.memset(bias_row[:].bitcast(F32), 0.0)
-        nc.vector.memset(warm_in[:], 0.0)
         nc.vector.memset(zeros[:], 0.0)
-        nc.vector.memset(w_scales[:].bitcast(I32), 0)
-        nc.vector.memset(ones[:], 1.0)
-        nc.vector.tensor_copy(out=ident_bf16[:], in_=ident_f32[:])
+        nc.vector.memset(ident_f32[:], 0.0)
+        nc.gpsimd.memset(w_scales[:].bitcast(I32), 0)
+        make_identity(nc, ident_f32[:], nomemset=True)
+        nc.gpsimd.memset(bias_row[:].bitcast(F32), 0.0)
+        nc.vector.memset(warm_in[:], 0.0)
         warm_up()
-        nc.sync.dma_start(out=h_sb[:, 0:PAIR, :], in_=h_rows[:, 0:PAIR, :])
+        nc.vector.tensor_copy(out=ident_bf16[:], in_=ident_f32[:])
+        nc.scalar.dma_start(out=h_sb[:, 0:PAIR, :], in_=h_rows[:, 0:PAIR, :])
         nc.scalar.dma_start(out=c_sb[:, 0:PAIR, :], in_=c_rows[:, 0:PAIR, :])
-        nc.scalar.dma_start(out=bias_row[0:1, COL_A], in_=alpha_bias.unsqueeze(0))
-        nc.scalar.dma_start(out=c_sb[:, PAIR:ROW_TILES, :], in_=c_rows[:, PAIR:ROW_TILES, :])
+        nc.scalar.dma_start(out=w_plain[:, COL_IOG], in_=weight_hh)
         load_table()
-        nc.sync.dma_start(out=w_plain[:, COL_A], in_=alpha_weight_hh)
-        nc.sync.dma_start(out=w_plain[:, COL_IOG], in_=weight_hh)
         nc.sync.dma_start(out=h_sb[:, PAIR:ROW_TILES, :], in_=h_rows[:, PAIR:ROW_TILES, :])
-        nc.sync.dma_start(out=bias_row[0:1, COL_IOG], in_=bias.unsqueeze(0))
+        nc.sync.dma_start(out=w_plain[:, COL_A], in_=alpha_weight_hh)
+        nc.sync.dma_start(out=c_sb[:, PAIR:ROW_TILES, :], in_=c_rows[:, PAIR:ROW_TILES, :])
         load_scale(alpha_weight_ih_scales, COL_A, 0)
+        load_x(nc.sync, 0)
         load_scale(alpha_weight_ih_scales, COL_A, 1)
         load_scale(alpha_weight_ih_scales, COL_A, 2)
-        load_scale(alpha_weight_ih_scales, COL_A, 3)
-        nc.sync.dma_start(
-            out=w_words[:, 2 * H : 2 * GATES].bitcast(I32), in_=weight_ih_words[0].bitcast(I32)
-        )
         nc.sync.dma_start(
             out=w_words[:, 0 : 2 * H].bitcast(I32), in_=alpha_weight_ih_words[0].bitcast(I32)
         )
+        nc.sync.dma_start(
+            out=w_words[:, 2 * H : 2 * GATES].bitcast(I32), in_=weight_ih_words[0].bitcast(I32)
+        )
+        load_scale(alpha_weight_ih_scales, COL_A, 3)
         load_scale(weight_ih_scales, COL_IOG, 0)
+        load_x(nc.sync, 1)
         load_scale(weight_ih_scales, COL_IOG, 1)
         load_scale(weight_ih_scales, COL_IOG, 2)
         load_scale(weight_ih_scales, COL_IOG, 3)
+        nc.sync.dma_start(out=bias_row[0:1, COL_IOG], in_=bias.unsqueeze(0))
+        nc.sync.dma_start(out=bias_row[0:1, COL_A], in_=alpha_bias.unsqueeze(0))
 
-        bias_ai = keep.tile([P, PAIR, 2 * H], F32)
-        bias_t = keep.tile([P, 2], F32)
+        bias_t = keep.tile([P, 4], F32)
+        minus_bias_a = keep.tile([P, 1], F32)
+        minus_one = keep.tile([P, 1], F32)
+        nc.vector.memset(minus_one[:], -1.0)
         x_codes = keep.tile([P, B], U32, align_bytes=64)
         x_scales = keep.tile([P, B], U8, align_bytes=64)
-        og_t = [keep.tile([P, B], F32, name="og_t%d" % n) for n in range(2)]
-        og = [keep.tile([P, ROW_TILES, H], F32, name="og%d" % n) for n in range(2)]
+        g_t = keep.tile([P, B], F32)
+        o_t = keep.tile([P, B], F32)
+        o_sb = keep.tile([P, ROW_TILES, H], F32)
         t = {}
+
+        def rows_of(first, tiles):
+            return slice(first * P, (first + tiles) * P)
+
+        def gate_cols(n):
+            return slice(n * H, (n + 1) * H)
 
         def tiles_of(p):
             return slice(p * PAIR, (p + 1) * PAIR)
 
-        def spread_biases():
-            for a, copy in enumerate((nc.vector.tensor_copy, nc.scalar.copy)):
-                bias_ps = banks.tile([P, 2 * H], F32, name="bias_ps", tag="bank")
-                nc.tensor.matmul(out=bias_ps[:], lhsT=ones[:], rhs=bias_row[:, COL_AI], start=True, stop=True)
-                copy(out=bias_ai[:, a, :], in_=bias_ps[:])
-
         def turn_biases():
-            bias_ps = banks.tile([P, 2, P], BF16, name="bias_t_ps", tag="bank")
-            for n, cols in enumerate((COL_O, COL_G)):
-                nc.tensor.transpose(out=bias_ps[:, n, :], in_=bias_row[:, cols], identity=ident_bf16[:])
+            bias_ps = banks.tile([P, 4, P], BF16, name="bias_ps", tag="bank")
+            for n in range(4):
+                nc.tensor.transpose(out=bias_ps[:, n, :], in_=bias_row[:, gate_cols(n)], identity=ident_bf16[:])
             nc.vector.tensor_copy(out=bias_t[:], in_=bias_ps[:, :, 0])
+            nc.vector.tensor_scalar(
+                out=minus_bias_a[:], in0=bias_t[:, ALPHA : ALPHA + 1], scalar1=-1.0, scalar2=None, op0=ALU.mult
+            )
 
-        def turn_hc(p, copy):
-            hc_ps = banks.tile([P, PAIR, 2, P], BF16, name="hc_ps", tag="bank")
-            for a in range(PAIR):
-                for which, rows_sb in enumerate((h_sb, c_sb)):
+        def turn_hc(p):
+            t["hc_ps", p] = banks.tile([P, 2, PAIR, P], BF16, name="hc_ps", tag="bank")
+            for which, rows_sb in enumerate((h_sb, c_sb)):
+                for a in range(PAIR):
                     nc.tensor.transpose(
-                        out=hc_ps[:, a, which, :], in_=rows_sb[:, p * PAIR + a, :], identity=ident_bf16[:]
+                        out=t["hc_ps", p][:, which, a, :], in_=rows_sb[:, p * PAIR + a, :], identity=ident_bf16[:]
                     )
-            t["hc", p] = keep.tile([P, PAIR, 2, P], BF16, name="hc%d" % p)
-            copy(out=t["hc", p][:], in_=hc_ps[:])
 
-        def plain_ai(p):
-            plain_ps = banks.tile([P, PAIR, 2 * H], F32, name="plain_ps", tag="bank")
-            for a in range(PAIR):
-                for which, cols in ((0, COL_I), (1, COL_A)):
-                    nc.tensor.matmul(
-                        out=plain_ps[:, a, cols],
-                        lhsT=t["hc", p][:, a, which, :],
-                        rhs=w_plain[:, cols],
-                        start=True,
-                        stop=True,
-                    )
-            t["plain", p] = keep.tile([P, PAIR, 2 * H], F32, name="plain%d" % p)
-            nc.vector.tensor_tensor(out=t["plain", p][:], in0=plain_ps[:], in1=bias_ai[:], op=ALU.add)
+        def move_hc(p, copy):
+            t["hc", p] = keep.tile([P, 2, PAIR, P], BF16, name="hc%d" % p)
+            copy(out=t["hc", p][:], in_=t["hc_ps", p][:])
+
+        def minus_c_scalar(p):
+            t["minus_c", p] = keep.tile([P, PAIR, P], F32, name="minus_c%d" % p)
+            nc.scalar.activation(out=t["minus_c", p][:], in_=t["hc", p][:, 1, :, :], func=ACT.Copy, scale=-1.0)
+
+        def minus_c_vector(p):
+            t["minus_c", p] = keep.tile([P, PAIR, P], F32, name="minus_c%d" % p)
+            nc.vector.tensor_scalar(
+                out=t["minus_c", p][:], in0=t["hc", p][:, 1, :, :], scalar1=-1.0, scalar2=None, op0=ALU.mult
+            )
+
+        def minus_c_gpsimd(p):
+            t["minus_c", p] = keep.tile([P, PAIR, P], F32, name="minus_c%d" % p)
+            nc.gpsimd.tensor_scalar(
+                out=t["minus_c", p][:],
+                in0=t["hc", p][:, 1, :, :],
+                scalar1=-1.0,
+                scalar2=0.0,
+                op0=ALU.mult,
+                op1=ALU.add,
+            )
+
+        def plain_ai(p, copy):
+            plain_ps = banks.tile([P, 2, PAIR * P], F32, name="plain_ps", tag="bank")
+            for n, which in ((ALPHA, 1), (GATE_I, 0)):
+                nc.tensor.matmul(
+                    out=plain_ps[:, n, :],
+                    lhsT=w_plain[:, gate_cols(n)],
+                    rhs=t["hc", p][:, which, :, :].rearrange("k a b -> k (a b)"),
+                    start=True,
+                    stop=True,
+                )
+            t["plain", p] = keep.tile([P, 2, PAIR * P], F32, name="plain%d" % p)
+            copy(out=t["plain", p][:], in_=plain_ps[:])
+
+        def plain_g(block, copy):
+            first, tiles = BLOCKS[block]
+            plain_ps = banks.tile([P, tiles * P], F32, name="plain_g_ps", tag="bank")
+            for p in range(first // PAIR, (first + tiles) // PAIR):
+                nc.tensor.matmul(
+                    out=plain_ps[:, rows_of(p * PAIR - first, PAIR)],
+                    lhsT=w_plain[:, gate_cols(GATE_G)],
+                    rhs=t["hc", p][:, 0, :, :].rearrange("k a b -> k (a b)"),
+                    start=True,
+                    stop=True,
+                )
+            t["plain_g", block] = keep.tile([P, tiles * P], F32, name="plain_g%d" % block)
+            copy(out=t["plain_g", block][:], in_=plain_ps[:])
 
         def turn_x(p, copy):
             x_ps = banks.tile([P, PAIR, 2, P], F32, name="x_ps", tag="bank")
@@ -201,105 +241,124 @@ def tile_multiinputlstmcell_pa_s_kernel(
                 in_=t["grouped", p][:].rearrange("p b t -> p (b t)"),
             )
 
-        def mx_ai(p):
-            t["ai_ps", p] = banks.tile([P, PAIR, 2 * H], F32, name="ai_ps", tag="bank")
-            for a in range(PAIR):
-                rows = slice((p * PAIR + a) * P, (p * PAIR + a + 1) * P)
-                nc.tensor.matmul_mx(
-                    out=t["ai_ps", p][:, a, :],
-                    lhsT=x_codes[:, rows].bitcast(FP8X4),
-                    lhsT_scale=x_scales[:, rows],
-                    rhs=w_words[:, 0 : 4 * H].bitcast(FP4X4),
-                    rhs_scale=w_scales[:, COL_AI],
-                    start=True,
-                    stop=True,
-                )
-
-        def gates_ai(p):
-            pre = keep.tile([P, PAIR, 2 * H], F32, name="pre%d" % p)
-            nc.vector.tensor_tensor(out=pre[:], in0=t["ai_ps", p][:], in1=t["plain", p][:], op=ALU.add)
-            t["ai", p] = keep.tile([P, PAIR, 2 * H], F32, name="ai%d" % p)
-            nc.scalar.activation(out=t["ai", p][:], in_=pre[:], func=ACT.Sigmoid)
-
-        def mx_og(n, block):
-            first, tiles = BLOCKS[block]
-            cols = (COL_O, COL_G)[n]
-            rows = slice(first * P, (first + tiles) * P)
-            t["og_ps", n, block] = banks.tile([P, tiles * P], F32, name="og_ps", tag="bank")
+        def mx(out, n, rows):
             nc.tensor.matmul_mx(
-                out=t["og_ps", n, block][:],
-                lhsT=w_words[:, 2 * cols.start : 2 * cols.stop].bitcast(FP4X4),
-                lhsT_scale=w_scales[:, cols],
+                out=out,
+                lhsT=w_words[:, 2 * n * H : 2 * (n + 1) * H].bitcast(FP4X4),
+                lhsT_scale=w_scales[:, gate_cols(n)],
                 rhs=x_codes[:, rows].bitcast(FP8X4),
                 rhs_scale=x_scales[:, rows],
                 start=True,
                 stop=True,
             )
 
-        def copy_og_vector(n, block):
+        def mx_ai(p):
+            t["ai_ps", p] = banks.tile([P, 2, PAIR * P], F32, name="ai_ps", tag="bank")
+            for n in (ALPHA, GATE_I):
+                mx(t["ai_ps", p][:, n, :], n, rows_of(p * PAIR, PAIR))
+
+        def add_ai(p):
+            t["pre", p] = keep.tile([P, 2, PAIR * P], F32, name="pre%d" % p)
+            nc.vector.tensor_tensor(out=t["pre", p][:], in0=t["ai_ps", p][:], in1=t["plain", p][:], op=ALU.add)
+
+        def gates_ai(p):
+            t["ai", p] = keep.tile([P, 2, PAIR * P], F32, name="ai%d" % p)
+            nc.scalar.activation(
+                out=t["ai", p][:, GATE_I, :], in_=t["pre", p][:, GATE_I, :], func=ACT.Sigmoid, bias=bias_t[:, 1:2]
+            )
+            nc.scalar.activation(
+                out=t["ai", p][:, ALPHA, :],
+                in_=t["pre", p][:, ALPHA, :],
+                func=ACT.Sigmoid,
+                bias=minus_bias_a[:],
+                scale=-1.0,
+            )
+
+        def add_turned(out, first_in, second_in):
+            nc.tensor.matmul(out=out, lhsT=first_in, rhs=ident_f32[:], start=True, stop=False, is_transpose=True)
+            nc.tensor.matmul(out=out, lhsT=second_in, rhs=ident_f32[:], start=False, stop=True, is_transpose=True)
+
+        def difference(p):
+            t["d_ps", p] = banks.tile([P, PAIR, H], F32, name="d_ps", tag="bank")
+            for a in range(PAIR):
+                add_turned(
+                    t["d_ps", p][:, a, :], t["ai", p][:, GATE_I, rows_of(a, 1)], t["ai", p][:, ALPHA, rows_of(a, 1)]
+                )
+
+        def weight(p):
+            t["w", p] = keep.tile([P, PAIR, H], F32, name="w%d" % p)
+            nc.scalar.activation(out=t["w", p][:], in_=t["d_ps", p][:], func=ACT.Sigmoid, bias=minus_one[:])
+
+        def mx_g(block):
+            first, tiles = BLOCKS[block]
+            t["g_ps", block] = banks.tile([P, tiles * P], F32, name="g_ps", tag="bank")
+            mx(t["g_ps", block][:], GATE_G, rows_of(first, tiles))
+
+        def add_g(block):
+            first, tiles = BLOCKS[block]
+            t["pre_g", block] = keep.tile([P, tiles * P], F32, name="pre_g%d" % block)
+            nc.vector.tensor_tensor(
+                out=t["pre_g", block][:], in0=t["g_ps", block][:], in1=t["plain_g", block][:], op=ALU.add
+            )
+
+        def gate_g(block):
+            first, tiles = BLOCKS[block]
+            nc.scalar.activation(
+                out=g_t[:, rows_of(first, tiles)], in_=t["pre_g", block][:], func=ACT.Tanh, bias=bias_t[:, 3:4]
+            )
+
+        def g_minus_c(p):
+            t["e_ps", p] = banks.tile([P, PAIR, H], F32, name="e_ps", tag="bank")
+            for a in range(PAIR):
+                add_turned(t["e_ps", p][:, a, :], t["minus_c", p][:, a, :], g_t[:, rows_of(p * PAIR + a, 1)])
+
+        def mx_o(block):
+            first, tiles = BLOCKS[block]
+            t["o_ps", block] = banks.tile([P, tiles * P], F32, name="o_ps", tag="bank")
+            mx(t["o_ps", block][:], GATE_O, rows_of(first, tiles))
+
+        def copy_o_vector(block):
             first, tiles = BLOCKS[block]
             nc.vector.tensor_scalar(
-                out=og_t[n][:, first * P : (first + tiles) * P],
-                in0=t["og_ps", n, block][:],
-                scalar1=bias_t[:, n : n + 1],
+                out=o_t[:, rows_of(first, tiles)],
+                in0=t["o_ps", block][:],
+                scalar1=bias_t[:, 2:3],
                 scalar2=None,
                 op0=ALU.add,
             )
 
-        def copy_og_scalar(n, block):
+        def copy_o_scalar(block):
             first, tiles = BLOCKS[block]
             nc.scalar.activation(
-                out=og_t[n][:, first * P : (first + tiles) * P],
-                in_=t["og_ps", n, block][:],
-                func=ACT.Identity,
-                bias=bias_t[:, n : n + 1],
+                out=o_t[:, rows_of(first, tiles)], in_=t["o_ps", block][:], func=ACT.Identity, bias=bias_t[:, 2:3]
             )
 
-        def sum_og(n, block):
+        def sum_o(block):
             first, tiles = BLOCKS[block]
-            cols = (COL_O, COL_G)[n]
-            t["og_sum", n, block] = banks.tile([P, tiles, H], F32, name="og_sum", tag="bank")
+            t["o_sum", block] = banks.tile([P, tiles, H], F32, name="o_sum", tag="bank")
             for j in range(first, first + tiles):
-                out = t["og_sum", n, block][:, j - first, :]
-                nc.tensor.matmul(
-                    out=out, lhsT=t["hc", j // PAIR][:, j % PAIR, 0, :], rhs=w_plain[:, cols], start=True, stop=False
-                )
+                out = t["o_sum", block][:, j - first, :]
                 nc.tensor.matmul(
                     out=out,
-                    lhsT=og_t[n][:, j * P : (j + 1) * P],
-                    rhs=ident_f32[:],
-                    start=False,
-                    stop=True,
-                    is_transpose=True,
+                    lhsT=t["hc", j // PAIR][:, 0, j % PAIR, :],
+                    rhs=w_plain[:, gate_cols(GATE_O)],
+                    start=True,
+                    stop=False,
+                )
+                nc.tensor.matmul(
+                    out=out, lhsT=o_t[:, rows_of(j, 1)], rhs=ident_f32[:], start=False, stop=True, is_transpose=True
                 )
 
-        def gate_og(n, block):
+        def gate_o(block):
             first, tiles = BLOCKS[block]
-            nc.scalar.activation(
-                out=og[n][:, first : first + tiles, :],
-                in_=t["og_sum", n, block][:],
-                func=(ACT.Sigmoid, ACT.Tanh)[n],
-            )
+            nc.scalar.activation(out=o_sb[:, first : first + tiles, :], in_=t["o_sum", block][:], func=ACT.Sigmoid)
 
         def cell_tile(p, name):
             t[name, p] = keep.tile([P, PAIR, H], F32, name="%s%d" % (name, p))
             return t[name, p][:]
 
-        def i_minus_alpha(p):
-            nc.vector.tensor_tensor(
-                out=cell_tile(p, "d"), in0=t["ai", p][:, :, COL_I], in1=t["ai", p][:, :, COL_A], op=ALU.subtract
-            )
-
-        def weight(p):
-            nc.scalar.activation(out=cell_tile(p, "w"), in_=t["d", p][:], func=ACT.Sigmoid)
-
-        def g_minus_c(p):
-            nc.vector.tensor_tensor(
-                out=cell_tile(p, "e"), in0=og[1][:, tiles_of(p), :], in1=c_sb[:, tiles_of(p), :], op=ALU.subtract
-            )
-
         def weighted(p):
-            nc.vector.tensor_tensor(out=cell_tile(p, "m"), in0=t["w", p][:], in1=t["e", p][:], op=ALU.mult)
+            nc.vector.tensor_tensor(out=cell_tile(p, "m"), in0=t["e_ps", p][:], in1=t["w", p][:], op=ALU.mult)
 
         def add_c(p):
             nc.vector.tensor_tensor(out=cell_tile(p, "c1"), in0=t["m", p][:], in1=c_sb[:, tiles_of(p), :], op=ALU.add)
@@ -309,63 +368,72 @@ def tile_multiinputlstmcell_pa_s_kernel(
             nc.scalar.activation(out=cell_tile(p, "t"), in_=t["c1", p][:], func=ACT.Tanh)
 
         def output(p):
-            nc.vector.tensor_tensor(out=cell_tile(p, "h1"), in0=og[0][:, tiles_of(p), :], in1=t["t", p][:], op=ALU.mult)
+            nc.vector.tensor_tensor(out=cell_tile(p, "h1"), in0=o_sb[:, tiles_of(p), :], in1=t["t", p][:], op=ALU.mult)
             nc.sync.dma_start(out=h1_rows[:, tiles_of(p), :], in_=t["h1", p][:])
 
-        turn_hc(0, nc.vector.tensor_copy)
-        spread_biases()
-        turn_hc(1, nc.vector.tensor_copy)
-        turn_hc(2, nc.scalar.copy)
-        plain_ai(0)
-        plain_ai(1)
-        turn_x(0, nc.scalar.copy)
+        warm_up()
+        turn_hc(0)
+        move_hc(0, nc.vector.tensor_copy)
+        turn_hc(1)
+        move_hc(1, nc.vector.tensor_copy)
+        turn_hc(2)
+        move_hc(2, nc.scalar.copy)
+        minus_c_gpsimd(0)
+        minus_c_gpsimd(1)
+        minus_c_gpsimd(2)
+        plain_ai(0, nc.vector.tensor_copy)
+        plain_ai(1, nc.scalar.copy)
+        turn_x(0, nc.vector.tensor_copy)
+        plain_ai(2, nc.scalar.copy)
         turn_x(1, nc.scalar.copy)
-        turn_biases()
-        quantise(0)
-        plain_ai(2)
+        plain_g(0, nc.scalar.copy)
         turn_x(2, nc.scalar.copy)
-        quantise(1)
+        quantise(0)
         mx_ai(0)
-        mx_og(1, 0)
+        quantise(1)
+        add_ai(0)
+        turn_biases()
         gates_ai(0)
+        plain_g(1, nc.scalar.copy)
         mx_ai(1)
+        mx_g(0)
+        mx_o(0)
         quantise(2)
-        mx_og(1, 1)
-        mx_og(0, 0)
-        copy_og_vector(1, 0)
-        mx_ai(2)
-        sum_og(1, 0)
-        copy_og_scalar(1, 1)
+        add_ai(1)
         gates_ai(1)
-        i_minus_alpha(0)
-        weight(0)
-        gate_og(1, 0)
-        copy_og_vector(0, 0)
-        gates_ai(2)
-        i_minus_alpha(1)
+        difference(0)
+        add_g(0)
+        mx_o(1)
+        mx_ai(2)
+        copy_o_vector(0)
+        gate_g(0)
+        mx_g(1)
+        difference(1)
+        sum_o(0)
         g_minus_c(0)
-        g_minus_c(1)
-        sum_og(1, 1)
-        gate_og(1, 1)
-        i_minus_alpha(2)
+        weight(0)
+        add_ai(2)
+        add_g(1)
         weight(1)
-        mx_og(0, 1)
-        sum_og(0, 0)
+        gates_ai(2)
+        gate_g(1)
+        copy_o_vector(1)
+        g_minus_c(1)
         weighted(0)
-        copy_og_scalar(0, 1)
-        g_minus_c(2)
+        difference(2)
+        gate_o(0)
         weighted(1)
         weight(2)
-        sum_og(0, 1)
         add_c(0)
-        gate_og(0, 0)
-        weighted(2)
-        add_c(1)
         tanh_c1(0)
-        gate_og(0, 1)
-        add_c(2)
+        g_minus_c(2)
+        add_c(1)
         tanh_c1(1)
-        output(0)
+        sum_o(1)
+        weighted(2)
+        gate_o(1)
+        add_c(2)
         tanh_c1(2)
+        output(0)
         output(1)
         output(2)

@@ -24,8 +24,7 @@ GATES = 4 * H
 ALPHA, GATE_I, GATE_O, GATE_G = range(4)
 BLOCKS = ((0, 4), (4, 2))
 X_LOADS = ((0, 4), (4, 2))
-WARM_COLUMNS = 256
-WARM_MATMULS = 1
+WARM_MATMULS = 4
 
 FLOPS = 2 * B * I * GATES + 2 * B * H * GATES
 
@@ -68,7 +67,7 @@ def tile_multiinputlstmcell_pa_s_kernel(
         ident_f32 = keep.tile([P, P], F32)
         warm_in = keep.tile([P, 1], F32)
         w_scales = keep.tile([P, GATES], U8, align_bytes=64)
-        zeros = keep.tile([P, WARM_COLUMNS], F32)
+        zeros = keep.tile([P, P], F32)
         ident_bf16 = keep.tile([P, P], BF16)
         x_parts = [keep.tile([P, tiles, I], BF16, name="x_part%d" % s) for s, (first, tiles) in enumerate(X_LOADS)]
         x_sb = [x_parts[s][:, a, :] for s, (first, tiles) in enumerate(X_LOADS) for a in range(tiles)]
@@ -92,8 +91,9 @@ def tile_multiinputlstmcell_pa_s_kernel(
             nc.scalar.activation(out=warm_out[:], in_=warm_in[:], func=ACT.Sigmoid)
 
         def warm_up():
-            warm_ps = banks.tile([P, WARM_COLUMNS], F32, name="warm_ps", tag="bank")
-            nc.tensor.matmul(out=warm_ps[:], lhsT=zeros[:, 0:P], rhs=zeros[:], start=True, stop=True)
+            warm_ps = banks.tile([P, P], F32, name="warm_ps", tag="bank")
+            for i in range(WARM_MATMULS):
+                nc.tensor.matmul(out=warm_ps[:], lhsT=zeros[:], rhs=zeros[:], start=True, stop=True)
 
         nc.vector.memset(zeros[:], 0.0)
         nc.vector.memset(ident_f32[:], 0.0)
@@ -103,26 +103,24 @@ def tile_multiinputlstmcell_pa_s_kernel(
         nc.vector.memset(warm_in[:], 0.0)
         warm_up()
         nc.vector.tensor_copy(out=ident_bf16[:], in_=ident_f32[:])
-        nc.scalar.dma_start(out=h_sb[:, 0:PAIR, :], in_=h_rows[:, 0:PAIR, :])
-        nc.scalar.dma_start(out=c_sb[:, 0:PAIR, :], in_=c_rows[:, 0:PAIR, :])
+        nc.scalar.dma_start(out=c_sb[:], in_=c_rows)
+        nc.sync.dma_start(out=h_sb[:], in_=h_rows)
         nc.scalar.dma_start(out=w_plain[:, COL_IOG], in_=weight_hh)
         load_table()
-        nc.sync.dma_start(out=h_sb[:, PAIR:ROW_TILES, :], in_=h_rows[:, PAIR:ROW_TILES, :])
         nc.sync.dma_start(out=w_plain[:, COL_A], in_=alpha_weight_hh)
-        nc.sync.dma_start(out=c_sb[:, PAIR:ROW_TILES, :], in_=c_rows[:, PAIR:ROW_TILES, :])
         load_scale(alpha_weight_ih_scales, COL_A, 0)
         load_x(nc.sync, 0)
         load_scale(alpha_weight_ih_scales, COL_A, 1)
         load_scale(alpha_weight_ih_scales, COL_A, 2)
+        load_scale(alpha_weight_ih_scales, COL_A, 3)
         nc.sync.dma_start(
             out=w_words[:, 0 : 2 * H].bitcast(I32), in_=alpha_weight_ih_words[0].bitcast(I32)
         )
         nc.sync.dma_start(
             out=w_words[:, 2 * H : 2 * GATES].bitcast(I32), in_=weight_ih_words[0].bitcast(I32)
         )
-        load_scale(alpha_weight_ih_scales, COL_A, 3)
-        load_scale(weight_ih_scales, COL_IOG, 0)
         load_x(nc.sync, 1)
+        load_scale(weight_ih_scales, COL_IOG, 0)
         load_scale(weight_ih_scales, COL_IOG, 1)
         load_scale(weight_ih_scales, COL_IOG, 2)
         load_scale(weight_ih_scales, COL_IOG, 3)
@@ -155,7 +153,7 @@ def tile_multiinputlstmcell_pa_s_kernel(
                 nc.tensor.transpose(out=bias_ps[:, n, :], in_=bias_row[:, gate_cols(n)], identity=ident_bf16[:])
             nc.vector.tensor_copy(out=bias_t[:], in_=bias_ps[:, :, 0])
             nc.vector.tensor_scalar(
-                out=minus_bias_a[:], in0=bias_t[:, ALPHA : ALPHA + 1], scalar1=-1.0, scalar2=None, op0=ALU.mult
+                out=minus_bias_a[:], in0=bias_ps[:, ALPHA, 0:1], scalar1=-1.0, scalar2=None, op0=ALU.mult
             )
 
         def turn_hc(p):
@@ -357,21 +355,27 @@ def tile_multiinputlstmcell_pa_s_kernel(
             t[name, p] = keep.tile([P, PAIR, H], F32, name="%s%d" % (name, p))
             return t[name, p][:]
 
+        c1_sb = keep.tile([P, ROW_TILES, H], F32)
+
         def weighted(p):
             nc.vector.tensor_tensor(out=cell_tile(p, "m"), in0=t["e_ps", p][:], in1=t["w", p][:], op=ALU.mult)
 
         def add_c(p):
-            nc.vector.tensor_tensor(out=cell_tile(p, "c1"), in0=t["m", p][:], in1=c_sb[:, tiles_of(p), :], op=ALU.add)
-            nc.sync.dma_start(out=c1_rows[:, tiles_of(p), :], in_=t["c1", p][:])
+            nc.vector.tensor_tensor(
+                out=c1_sb[:, tiles_of(p), :], in0=t["m", p][:], in1=c_sb[:, tiles_of(p), :], op=ALU.add
+            )
+            for first, tiles in BLOCKS:
+                if first + tiles == (p + 1) * PAIR:
+                    block = slice(first, first + tiles)
+                    nc.sync.dma_start(out=c1_rows[:, block, :], in_=c1_sb[:, block, :])
 
         def tanh_c1(p):
-            nc.scalar.activation(out=cell_tile(p, "t"), in_=t["c1", p][:], func=ACT.Tanh)
+            nc.scalar.activation(out=cell_tile(p, "t"), in_=c1_sb[:, tiles_of(p), :], func=ACT.Tanh)
 
         def output(p):
             nc.vector.tensor_tensor(out=cell_tile(p, "h1"), in0=o_sb[:, tiles_of(p), :], in1=t["t", p][:], op=ALU.mult)
             nc.sync.dma_start(out=h1_rows[:, tiles_of(p), :], in_=t["h1", p][:])
 
-        warm_up()
         turn_hc(0)
         move_hc(0, nc.vector.tensor_copy)
         turn_hc(1)

from contextlib import ExitStack

import concourse.mybir as mybir
from concourse.masks import make_identity

F32 = mybir.dt.float32
BF16 = mybir.dt.bfloat16
I32 = mybir.dt.int32
U32 = mybir.dt.uint32
U8 = mybir.dt.uint8
FP8X4 = mybir.dt.float8_e4m3fn_x4
FP4X4 = mybir.dt.float4_e2m1fn_x4
ACT = mybir.ActivationFunctionType
ALU = mybir.AluOpType

P = 128
B = 768
I = 512
H = 128
ROW_TILES = B // P
PAIR = 2
PAIRS = ROW_TILES // PAIR
GATES = 4 * H
ALPHA, GATE_I, GATE_O, GATE_G = range(4)
BLOCKS = ((0, 4), (4, 2))
X_LOADS = ((0, 4), (4, 2))
WARM_MATMULS = 4

FLOPS = 2 * B * I * GATES + 2 * B * H * GATES


def tile_multiinputlstmcell_pa_s_kernel(
    tc,
    input_,
    c_input,
    h_0,
    weight_ih_words,
    weight_ih_scales,
    weight_hh,
    alpha_weight_ih_words,
    alpha_weight_ih_scales,
    alpha_weight_hh,
    bias,
    alpha_bias,
    out_0,
    out_1,
):
    nc = tc.nc
    COL_A = slice(0 * H, 1 * H)
    COL_I = slice(1 * H, 2 * H)
    COL_O = slice(2 * H, 3 * H)
    COL_G = slice(3 * H, 4 * H)
    COL_AI = slice(0 * H, 2 * H)
    COL_IOG = slice(1 * H, 4 * H)
    x_rows = input_.rearrange("(p j) k -> p j k", j=ROW_TILES)
    h_rows = h_0.rearrange("(p j) h -> p j h", j=ROW_TILES)
    c_rows = c_input.rearrange("(p j) o h -> p j (o h)", j=ROW_TILES)
    h1_rows = out_0.rearrange("(p j) h -> p j h", j=ROW_TILES)
    c1_rows = out_1.rearrange("(p j) h -> p j h", j=ROW_TILES)

    with ExitStack() as ctx:
        keep = ctx.enter_context(tc.tile_pool(name="keep", bufs=1))
        banks = ctx.enter_context(tc.psum_pool(name="banks", bufs=8))
        ctx.enter_context(tc.manual_schedule())

        bias_row = keep.tile([P, GATES], BF16)
        ident_f32 = keep.tile([P, P], F32)
        warm_in = keep.tile([P, 1], F32)
        w_scales = keep.tile([P, GATES], U8, align_bytes=64)
        zeros = keep.tile([P, P], F32)
        ident_bf16 = keep.tile([P, P], BF16)
        x_parts = [keep.tile([P, tiles, I], BF16, name="x_part%d" % s) for s, (first, tiles) in enumerate(X_LOADS)]
        x_sb = [x_parts[s][:, a, :] for s, (first, tiles) in enumerate(X_LOADS) for a in range(tiles)]
        h_sb = keep.tile([P, ROW_TILES, H], BF16)
        c_sb = keep.tile([P, ROW_TILES, H], BF16)
        w_plain = keep.tile([P, GATES], BF16)
        w_words = keep.tile([P, 2 * GATES], U8, align_bytes=64)
        warm_out = keep.tile([P, 1], F32)

        def load_x(engine, s):
            first, tiles = X_LOADS[s]
            engine.dma_start(out=x_parts[s][:], in_=x_rows[:, first : first + tiles, :])

        def load_scale(scales, cols, q):
            nc.sync.dma_start(
                out=w_scales[32 * q : 32 * q + 4, cols].bitcast(I32),
                in_=scales[0, 4 * q : 4 * q + 4, :].bitcast(I32),
            )

        def load_table():
            nc.scalar.activation(out=warm_out[:], in_=warm_in[:], func=ACT.Sigmoid)

        def warm_up():
            warm_ps = banks.tile([P, P], F32, name="warm_ps", tag="bank")
            for i in range(WARM_MATMULS):
                nc.tensor.matmul(out=warm_ps[:], lhsT=zeros[:], rhs=zeros[:], start=True, stop=True)

        nc.vector.memset(zeros[:], 0.0)
        nc.vector.memset(ident_f32[:], 0.0)
        nc.gpsimd.memset(w_scales[:].bitcast(I32), 0)
        make_identity(nc, ident_f32[:], nomemset=True)
        nc.gpsimd.memset(bias_row[:].bitcast(F32), 0.0)
        nc.vector.memset(warm_in[:], 0.0)
        warm_up()
        nc.vector.tensor_copy(out=ident_bf16[:], in_=ident_f32[:])
        nc.scalar.dma_start(out=c_sb[:], in_=c_rows)
        nc.sync.dma_start(out=h_sb[:], in_=h_rows)
        nc.scalar.dma_start(out=w_plain[:, COL_IOG], in_=weight_hh)
        load_table()
        nc.sync.dma_start(out=w_plain[:, COL_A], in_=alpha_weight_hh)
        load_scale(alpha_weight_ih_scales, COL_A, 0)
        load_x(nc.sync, 0)
        load_scale(alpha_weight_ih_scales, COL_A, 1)
        load_scale(alpha_weight_ih_scales, COL_A, 2)
        load_scale(alpha_weight_ih_scales, COL_A, 3)
        nc.sync.dma_start(
            out=w_words[:, 0 : 2 * H].bitcast(I32), in_=alpha_weight_ih_words[0].bitcast(I32)
        )
        nc.sync.dma_start(
            out=w_words[:, 2 * H : 2 * GATES].bitcast(I32), in_=weight_ih_words[0].bitcast(I32)
        )
        load_x(nc.sync, 1)
        load_scale(weight_ih_scales, COL_IOG, 0)
        load_scale(weight_ih_scales, COL_IOG, 1)
        load_scale(weight_ih_scales, COL_IOG, 2)
        load_scale(weight_ih_scales, COL_IOG, 3)
        nc.sync.dma_start(out=bias_row[0:1, COL_IOG], in_=bias.unsqueeze(0))
        nc.sync.dma_start(out=bias_row[0:1, COL_A], in_=alpha_bias.unsqueeze(0))

        bias_t = keep.tile([P, 4], F32)
        minus_bias_a = keep.tile([P, 1], F32)
        minus_one = keep.tile([P, 1], F32)
        nc.vector.memset(minus_one[:], -1.0)
        x_codes = keep.tile([P, B], U32, align_bytes=64)
        x_scales = keep.tile([P, B], U8, align_bytes=64)
        g_t = keep.tile([P, B], F32)
        o_t = keep.tile([P, B], F32)
        o_sb = keep.tile([P, ROW_TILES, H], F32)
        t = {}

        def rows_of(first, tiles):
            return slice(first * P, (first + tiles) * P)

        def gate_cols(n):
            return slice(n * H, (n + 1) * H)

        def tiles_of(p):
            return slice(p * PAIR, (p + 1) * PAIR)

        def turn_biases():
            bias_ps = banks.tile([P, 4, P], BF16, name="bias_ps", tag="bank")
            for n in range(4):
                nc.tensor.transpose(out=bias_ps[:, n, :], in_=bias_row[:, gate_cols(n)], identity=ident_bf16[:])
            nc.vector.tensor_copy(out=bias_t[:], in_=bias_ps[:, :, 0])
            nc.vector.tensor_scalar(
                out=minus_bias_a[:], in0=bias_ps[:, ALPHA, 0:1], scalar1=-1.0, scalar2=None, op0=ALU.mult
            )

        def turn_hc(p):
            t["hc_ps", p] = banks.tile([P, 2, PAIR, P], BF16, name="hc_ps", tag="bank")
            for which, rows_sb in enumerate((h_sb, c_sb)):
                for a in range(PAIR):
                    nc.tensor.transpose(
                        out=t["hc_ps", p][:, which, a, :], in_=rows_sb[:, p * PAIR + a, :], identity=ident_bf16[:]
                    )

        def move_hc(p, copy):
            t["hc", p] = keep.tile([P, 2, PAIR, P], BF16, name="hc%d" % p)
            copy(out=t["hc", p][:], in_=t["hc_ps", p][:])

        def minus_c_scalar(p):
            t["minus_c", p] = keep.tile([P, PAIR, P], F32, name="minus_c%d" % p)
            nc.scalar.activation(out=t["minus_c", p][:], in_=t["hc", p][:, 1, :, :], func=ACT.Copy, scale=-1.0)

        def minus_c_vector(p):
            t["minus_c", p] = keep.tile([P, PAIR, P], F32, name="minus_c%d" % p)
            nc.vector.tensor_scalar(
                out=t["minus_c", p][:], in0=t["hc", p][:, 1, :, :], scalar1=-1.0, scalar2=None, op0=ALU.mult
            )

        def minus_c_gpsimd(p):
            t["minus_c", p] = keep.tile([P, PAIR, P], F32, name="minus_c%d" % p)
            nc.gpsimd.tensor_scalar(
                out=t["minus_c", p][:],
                in0=t["hc", p][:, 1, :, :],
                scalar1=-1.0,
                scalar2=0.0,
                op0=ALU.mult,
                op1=ALU.add,
            )

        def plain_ai(p, copy):
            plain_ps = banks.tile([P, 2, PAIR * P], F32, name="plain_ps", tag="bank")
            for n, which in ((ALPHA, 1), (GATE_I, 0)):
                nc.tensor.matmul(
                    out=plain_ps[:, n, :],
                    lhsT=w_plain[:, gate_cols(n)],
                    rhs=t["hc", p][:, which, :, :].rearrange("k a b -> k (a b)"),
                    start=True,
                    stop=True,
                )
            t["plain", p] = keep.tile([P, 2, PAIR * P], F32, name="plain%d" % p)
            copy(out=t["plain", p][:], in_=plain_ps[:])

        def plain_g(block, copy):
            first, tiles = BLOCKS[block]
            plain_ps = banks.tile([P, tiles * P], F32, name="plain_g_ps", tag="bank")
            for p in range(first // PAIR, (first + tiles) // PAIR):
                nc.tensor.matmul(
                    out=plain_ps[:, rows_of(p * PAIR - first, PAIR)],
                    lhsT=w_plain[:, gate_cols(GATE_G)],
                    rhs=t["hc", p][:, 0, :, :].rearrange("k a b -> k (a b)"),
                    start=True,
                    stop=True,
                )
            t["plain_g", block] = keep.tile([P, tiles * P], F32, name="plain_g%d" % block)
            copy(out=t["plain_g", block][:], in_=plain_ps[:])

        def turn_x(p, copy):
            x_ps = banks.tile([P, PAIR, 2, P], F32, name="x_ps", tag="bank")
            for a in range(PAIR):
                x_words = x_sb[p * PAIR + a].bitcast(F32)
                for u in range(2):
                    nc.tensor.transpose(out=x_ps[:, a, u, :], in_=x_words[:, u : I // 2 : 2], identity=ident_f32[:])
            t["grouped", p] = keep.tile([P, PAIR * P, 4], BF16, name="grouped%d" % p, align_bytes=64)
            copy(
                out=t["grouped", p][:]
                .rearrange("p b t -> p (b t)")
                .bitcast(F32)
                .rearrange("p (a b u) -> p a b u", a=PAIR, u=2),
                in_=x_ps[:].rearrange("p a u b -> p a b u"),
            )

        def quantise(p):
            rows = slice(p * PAIR * P, (p + 1) * PAIR * P)
            nc.vector.quantize_mx(
                out=x_codes[:, rows].bitcast(FP8X4),
                scales=x_scales[:, rows],
                in_=t["grouped", p][:].rearrange("p b t -> p (b t)"),
            )

        def mx(out, n, rows):
            nc.tensor.matmul_mx(
                out=out,
                lhsT=w_words[:, 2 * n * H : 2 * (n + 1) * H].bitcast(FP4X4),
                lhsT_scale=w_scales[:, gate_cols(n)],
                rhs=x_codes[:, rows].bitcast(FP8X4),
                rhs_scale=x_scales[:, rows],
                start=True,
                stop=True,
            )

        def mx_ai(p):
            t["ai_ps", p] = banks.tile([P, 2, PAIR * P], F32, name="ai_ps", tag="bank")
            for n in (ALPHA, GATE_I):
                mx(t["ai_ps", p][:, n, :], n, rows_of(p * PAIR, PAIR))

        def add_ai(p):
            t["pre", p] = keep.tile([P, 2, PAIR * P], F32, name="pre%d" % p)
            nc.vector.tensor_tensor(out=t["pre", p][:], in0=t["ai_ps", p][:], in1=t["plain", p][:], op=ALU.add)

        def gates_ai(p):
            t["ai", p] = keep.tile([P, 2, PAIR * P], F32, name="ai%d" % p)
            nc.scalar.activation(
                out=t["ai", p][:, GATE_I, :], in_=t["pre", p][:, GATE_I, :], func=ACT.Sigmoid, bias=bias_t[:, 1:2]
            )
            nc.scalar.activation(
                out=t["ai", p][:, ALPHA, :],
                in_=t["pre", p][:, ALPHA, :],
                func=ACT.Sigmoid,
                bias=minus_bias_a[:],
                scale=-1.0,
            )

        def add_turned(out, first_in, second_in):
            nc.tensor.matmul(out=out, lhsT=first_in, rhs=ident_f32[:], start=True, stop=False, is_transpose=True)
            nc.tensor.matmul(out=out, lhsT=second_in, rhs=ident_f32[:], start=False, stop=True, is_transpose=True)

        def difference(p):
            t["d_ps", p] = banks.tile([P, PAIR, H], F32, name="d_ps", tag="bank")
            for a in range(PAIR):
                add_turned(
                    t["d_ps", p][:, a, :], t["ai", p][:, GATE_I, rows_of(a, 1)], t["ai", p][:, ALPHA, rows_of(a, 1)]
                )

        def weight(p):
            t["w", p] = keep.tile([P, PAIR, H], F32, name="w%d" % p)
            nc.scalar.activation(out=t["w", p][:], in_=t["d_ps", p][:], func=ACT.Sigmoid, bias=minus_one[:])

        def mx_g(block):
            first, tiles = BLOCKS[block]
            t["g_ps", block] = banks.tile([P, tiles * P], F32, name="g_ps", tag="bank")
            mx(t["g_ps", block][:], GATE_G, rows_of(first, tiles))

        def add_g(block):
            first, tiles = BLOCKS[block]
            t["pre_g", block] = keep.tile([P, tiles * P], F32, name="pre_g%d" % block)
            nc.vector.tensor_tensor(
                out=t["pre_g", block][:], in0=t["g_ps", block][:], in1=t["plain_g", block][:], op=ALU.add
            )

        def gate_g(block):
            first, tiles = BLOCKS[block]
            nc.scalar.activation(
                out=g_t[:, rows_of(first, tiles)], in_=t["pre_g", block][:], func=ACT.Tanh, bias=bias_t[:, 3:4]
            )

        def g_minus_c(p):
            t["e_ps", p] = banks.tile([P, PAIR, H], F32, name="e_ps", tag="bank")
            for a in range(PAIR):
                add_turned(t["e_ps", p][:, a, :], t["minus_c", p][:, a, :], g_t[:, rows_of(p * PAIR + a, 1)])

        def mx_o(block):
            first, tiles = BLOCKS[block]
            t["o_ps", block] = banks.tile([P, tiles * P], F32, name="o_ps", tag="bank")
            mx(t["o_ps", block][:], GATE_O, rows_of(first, tiles))

        def copy_o_vector(block):
            first, tiles = BLOCKS[block]
            nc.vector.tensor_scalar(
                out=o_t[:, rows_of(first, tiles)],
                in0=t["o_ps", block][:],
                scalar1=bias_t[:, 2:3],
                scalar2=None,
                op0=ALU.add,
            )

        def copy_o_scalar(block):
            first, tiles = BLOCKS[block]
            nc.scalar.activation(
                out=o_t[:, rows_of(first, tiles)], in_=t["o_ps", block][:], func=ACT.Identity, bias=bias_t[:, 2:3]
            )

        def sum_o(block):
            first, tiles = BLOCKS[block]
            t["o_sum", block] = banks.tile([P, tiles, H], F32, name="o_sum", tag="bank")
            for j in range(first, first + tiles):
                out = t["o_sum", block][:, j - first, :]
                nc.tensor.matmul(
                    out=out,
                    lhsT=t["hc", j // PAIR][:, 0, j % PAIR, :],
                    rhs=w_plain[:, gate_cols(GATE_O)],
                    start=True,
                    stop=False,
                )
                nc.tensor.matmul(
                    out=out, lhsT=o_t[:, rows_of(j, 1)], rhs=ident_f32[:], start=False, stop=True, is_transpose=True
                )

        def gate_o(block):
            first, tiles = BLOCKS[block]
            nc.scalar.activation(out=o_sb[:, first : first + tiles, :], in_=t["o_sum", block][:], func=ACT.Sigmoid)

        def cell_tile(p, name):
            t[name, p] = keep.tile([P, PAIR, H], F32, name="%s%d" % (name, p))
            return t[name, p][:]

        c1_sb = keep.tile([P, ROW_TILES, H], F32)

        def weighted(p):
            nc.vector.tensor_tensor(out=cell_tile(p, "m"), in0=t["e_ps", p][:], in1=t["w", p][:], op=ALU.mult)

        def add_c(p):
            nc.vector.tensor_tensor(
                out=c1_sb[:, tiles_of(p), :], in0=t["m", p][:], in1=c_sb[:, tiles_of(p), :], op=ALU.add
            )
            for first, tiles in BLOCKS:
                if first + tiles == (p + 1) * PAIR:
                    block = slice(first, first + tiles)
                    nc.sync.dma_start(out=c1_rows[:, block, :], in_=c1_sb[:, block, :])

        def tanh_c1(p):
            nc.scalar.activation(out=cell_tile(p, "t"), in_=c1_sb[:, tiles_of(p), :], func=ACT.Tanh)

        def output(p):
            nc.vector.tensor_tensor(out=cell_tile(p, "h1"), in0=o_sb[:, tiles_of(p), :], in1=t["t", p][:], op=ALU.mult)
            nc.sync.dma_start(out=h1_rows[:, tiles_of(p), :], in_=t["h1", p][:])

        turn_hc(0)
        move_hc(0, nc.vector.tensor_copy)
        turn_hc(1)
        move_hc(1, nc.vector.tensor_copy)
        turn_hc(2)
        move_hc(2, nc.scalar.copy)
        minus_c_gpsimd(0)
        minus_c_gpsimd(1)
        minus_c_gpsimd(2)
        plain_ai(0, nc.vector.tensor_copy)
        plain_ai(1, nc.scalar.copy)
        turn_x(0, nc.vector.tensor_copy)
        plain_ai(2, nc.scalar.copy)
        turn_x(1, nc.scalar.copy)
        plain_g(0, nc.scalar.copy)
        turn_x(2, nc.scalar.copy)
        quantise(0)
        mx_ai(0)
        quantise(1)
        add_ai(0)
        turn_biases()
        gates_ai(0)
        plain_g(1, nc.scalar.copy)
        mx_ai(1)
        mx_g(0)
        mx_o(0)
        quantise(2)
        add_ai(1)
        gates_ai(1)
        difference(0)
        add_g(0)
        mx_o(1)
        mx_ai(2)
        copy_o_vector(0)
        gate_g(0)
        mx_g(1)
        difference(1)
        sum_o(0)
        g_minus_c(0)
        weight(0)
        add_ai(2)
        add_g(1)
        weight(1)
        gates_ai(2)
        gate_g(1)
        copy_o_vector(1)
        g_minus_c(1)
        weighted(0)
        difference(2)
        gate_o(0)
        weighted(1)
        weight(2)
        add_c(0)
        tanh_c1(0)
        g_minus_c(2)
        add_c(1)
        tanh_c1(1)
        sum_o(1)
        weighted(2)
        gate_o(1)
        add_c(2)
        tanh_c1(2)
        output(0)
        output(1)
        output(2)
